import numpy as np
import ml_dtypes


def mxq(x, axis, fmt="e4m3"):
    dtype, down = {"e4m3": (ml_dtypes.float8_e4m3fn, 7), "e5m2": (ml_dtypes.float8_e5m2, 14)}[fmt]
    v = np.moveaxis(np.asarray(x, np.float32).astype(ml_dtypes.bfloat16).astype(np.float64), axis, -1)
    blocks = v.reshape(v.shape[:-1] + (-1, 32))
    amax = np.abs(blocks).max(-1, keepdims=True)
    byte = np.maximum(np.where(amax > 0, np.frexp(amax)[1] - 1 + 127, 0) - down, 1)
    scale = np.exp2(byte - 127.0)
    codes = (blocks / scale).astype(np.float32).astype(dtype).astype(np.float64)
    return np.moveaxis((codes * scale).reshape(v.shape), -1, axis)


WIDE = False


def mx_kscale(k):
    if not WIDE:
        return np.ones(k)
    levels = np.array([10, -10, 5, -5, 0])
    a = np.random.permutation(np.resize(levels, k // 512 * 4)).reshape(k // 512, 4)
    idx = np.arange(k)
    return np.exp2(a[idx // 512, idx % 128 // 32])


BF16 = ml_dtypes.bfloat16


def bf(x):
    return np.asarray(x, np.float32).astype(BF16)


def f64(x):
    return np.asarray(x).astype(np.float64)


B, N, C0, C1, C2, O0, O1, O2 = 16, 16, 512, 512, 512, 512, 2048, 512
G = C1 + C2
K = 2 * G


def sigmoid(v):
    return 1.0 / (1.0 + np.exp(-v))


def setup_inputs():
    s = mx_kscale(G)
    ss = np.concatenate([s, s])
    return {"x1": bf(np.random.random((B, N, C1)) * s[:C1]),
            "x2": bf(np.random.random((B, N, N, C2)) * s[C1:]),
            "W2": bf(np.random.standard_normal((K, O2)) * 2.0 / np.sqrt(K) / ss[:, None]),
            "b2": bf(np.random.standard_normal(O2) * 0.3)}


def reference(x1, x2, W2, b2):
    x1, x2 = f64(x1), f64(x2)
    e1 = np.broadcast_to(x1[:, :, None, :], (B, N, N, C1))
    g = np.concatenate([e1, x2], axis=-1)
    f2 = np.concatenate([g, np.swapaxes(g, 1, 2)], axis=-1)
    return sigmoid((mxq(f2, 3, "e4m3") @ mxq(f64(W2), 0, "e4m3")) + f64(b2))

@@ -1,0 +1,255 @@
+from contextlib import ExitStack
+
+import concourse.mybir as mybir
+from concourse.masks import make_identity
+
+F32 = mybir.dt.float32
+BF16 = mybir.dt.bfloat16
+U32 = mybir.dt.uint32
+I32 = mybir.dt.int32
+U8 = mybir.dt.uint8
+FP8X4 = mybir.dt.float8_e4m3fn_x4
+ADD = mybir.AluOpType.add
+SIGMOID = mybir.ActivationFunctionType.Sigmoid
+
+P = 128
+NB = 16
+NO = 16
+CH = 512
+OUT = 512
+HB = 8
+SLAB = 4
+NSLAB = NO // SLAB
+STORE_J = 4
+ACC_BUFS = 6
+
+FLOPS = 2 * NB * NO * NO * 4 * CH * OUT
+
+G_A, G_P, G_C, G_Q = 0, 1, 2, 3
+
+
+def tile_differentiablelogicmachine_pa_kernel(tc, x1, x2, W2, b2, out):
+    nc = tc.nc
+    with ExitStack() as ctx:
+        keep = ctx.enter_context(tc.tile_pool(name="keep", bufs=1))
+        grp_pool = ctx.enter_context(tc.tile_pool(name="grp", bufs=3))
+        res_pool = ctx.enter_context(tc.tile_pool(name="res", bufs=3))
+        tp_pool = ctx.enter_context(tc.psum_pool(name="tp", bufs=2))
+        acc_pool = ctx.enter_context(tc.psum_pool(name="acc", bufs=ACC_BUFS))
+
+        ident = keep.tile([P, P], F32, name="ident")
+        ones = keep.tile([P, P], BF16, name="ones")
+        b2row = keep.tile([P, OUT], BF16, name="b2row")
+        b2all = keep.tile([P, OUT], F32, name="b2all")
+        warm = keep.tile([P, 2], F32, name="warm")
+        x1_sb = keep.tile([P, 2, CH], BF16, name="x1_sb")
+        x1_grp = keep.tile([P, 2, P, 4], BF16, name="x1_grp", align_bytes=64)
+        x1_codes = keep.tile([P, 2, P], U32, name="x1_codes", align_bytes=64)
+        x1_scales = keep.tile([P, 2, P], U8, name="x1_scales", align_bytes=64)
+        w_raw = [keep.tile([P, 4, OUT], BF16, name="w_raw%d" % g) for g in range(4)]
+        w_grp = [keep.tile([P, OUT, 4], BF16, name="w_grp%d" % g, align_bytes=64) for g in range(4)]
+        w_codes = keep.tile([P, 4, OUT], U32, name="w_codes", align_bytes=64)
+        w_scales = keep.tile([P, 4, OUT], U8, name="w_scales", align_bytes=64)
+        x2_sb = [
+            [keep.tile([P, SLAB, CH], BF16, name="x2_sb%d_%d" % (h, s)) for s in range(NSLAB)]
+            for h in range(2)
+        ]
+        p_codes = [keep.tile([P, NO, P], U32, name="p_codes%d" % h, align_bytes=64) for h in range(2)]
+        p_scales = [keep.tile([P, NO, P], U8, name="p_scales%d" % h, align_bytes=64) for h in range(2)]
+        q_codes = [keep.tile([P, NO, P], U32, name="q_codes%d" % h, align_bytes=64) for h in range(2)]
+        q_scales = [keep.tile([P, NO, P], U8, name="q_scales%d" % h, align_bytes=64) for h in range(2)]
+        c_codes = [keep.tile([P, NO, P], U32, name="c_codes%d" % h, align_bytes=64) for h in range(2)]
+        c_scales = [keep.tile([P, NO, P], U8, name="c_scales%d" % h, align_bytes=64) for h in range(2)]
+        aprime = [keep.tile([P, OUT], F32, name="aprime%d" % h) for h in range(2)]
+
+        x1_v = x1.rearrange("(h b) i k -> h i b k", h=2)
+        x2_v = x2.rearrange("(h b) i j k -> h i b (j k)", h=2)
+        w_v = W2.rearrange("(g u p e) o -> g p u (e o)", g=4, u=2, e=2)
+        out_v = out.rearrange("(h b) i j o -> h i b (j o)", h=2)
+
+        def load_w(g):
+            nc.sync.dma_start(out=w_raw[g][:].rearrange("p (u e) o -> p u (e o)", u=2), in_=w_v[g])
+
+        def load_x2(h, s):
+            nc.sync.dma_start(
+                out=x2_sb[h][s][:].rearrange("p j k -> p (j k)"),
+                in_=x2_v[h][:, :, s * SLAB * CH : (s + 1) * SLAB * CH],
+            )
+
+        nc.vector.memset(b2row[:], 0.0)
+        nc.scalar.dma_start(out=b2row[0:1, :], in_=b2.unsqueeze(0))
+        for h in range(2):
+            nc.sync.dma_start(out=x1_sb[:, h, :], in_=x1_v[h])
+        load_w(G_P)
+        load_x2(0, 0)
+        load_w(G_C)
+        load_x2(0, 1)
+        load_x2(0, 2)
+        load_w(G_Q)
+        load_x2(0, 3)
+        load_w(G_A)
+        for s in range(NSLAB):
+            load_x2(1, s)
+
+        make_identity(nc, ident[:])
+        nc.vector.memset(ones[:], 1.0)
+        nc.vector.memset(warm[:], 0.0)
+        nc.scalar.activation(out=warm[:, 1:2], in_=warm[:, 0:1], func=SIGMOID)
+        nc.vector.memset(x1_scales[:].bitcast(I32), 0)
+        for h in range(2):
+            nc.vector.memset(p_scales[h][:].bitcast(I32), 0)
+
+        def regroup_w(g, engine):
+            dst = w_grp[g][:].rearrange("p (c i) t -> p c t i", i=4)
+            src = w_raw[g][:].rearrange("p t (c i) -> p c t i", i=4)
+            if engine == "v":
+                nc.vector.tensor_copy(out=dst, in_=src)
+            else:
+                nc.scalar.copy(out=dst, in_=src)
+
+        def quant_w(g):
+            nc.vector.quantize_mx(
+                out=w_codes[:, g, :].bitcast(FP8X4),
+                scales=w_scales[:, g, :],
+                in_=w_grp[g][:].rearrange("p o t -> p (o t)"),
+            )
+
+        def transpose_pair(src_words, dst_grp_words):
+            tp = tp_pool.tile([P, 2, 2, P], F32, name="tp", tag="tp")
+            for jj in range(2):
+                for u in range(2):
+                    nc.tensor.transpose(tp[:, jj, u, :], src_words[jj][:, u * P : (u + 1) * P], ident[:])
+            nc.scalar.copy(out=dst_grp_words, in_=tp[:].rearrange("p j u r -> p j r u"))
+
+        def slab(h, s):
+            words = x2_sb[h][s][:].bitcast(F32)
+            grp = grp_pool.tile([P, SLAB, P, 4], BF16, name="x2_grp", tag="x2_grp", align_bytes=64)
+            grp_words = grp[:].bitcast(F32)
+            for half in range(SLAB // 2):
+                transpose_pair(
+                    [words[:, 2 * half + jj, :] for jj in range(2)],
+                    grp_words[:, 2 * half : 2 * half + 2, :, :],
+                )
+            lo, hi = s * SLAB, (s + 1) * SLAB
+            nc.vector.quantize_mx(
+                out=p_codes[h][:, lo:hi, :].rearrange("p j r -> p (j r)").bitcast(FP8X4),
+                scales=p_scales[h][:, lo:hi, :].rearrange("p j r -> p (j r)"),
+                in_=grp[:].rearrange("p j r t -> p (j r t)"),
+            )
+
+        def q_moves(h, s):
+            lo, hi = s * SLAB, (s + 1) * SLAB
+            nc.vector.tensor_copy(
+                out=q_codes[h][:].bitcast(I32).rearrange("p j (i b) -> p j i b", b=HB)[:, :, lo:hi, :],
+                in_=p_codes[h][:].bitcast(I32).rearrange("p i (j b) -> p j i b", b=HB)[:, :, lo:hi, :],
+            )
+            nc.vector.tensor_copy(
+                out=q_scales[h][:].bitcast(I32).rearrange("p j (i w) -> p j i w", w=2)[:, :, lo:hi, :],
+                in_=p_scales[h][:].bitcast(I32).rearrange("p i (j w) -> p j i w", w=2)[:, :, lo:hi, :],
+            )
+
+        def c_moves(h):
+            nc.vector.tensor_copy(
+                out=c_codes[h][:].bitcast(I32).rearrange("p j (i b) -> p j i b", b=HB),
+                in_=x1_codes[:, h, :].bitcast(I32).rearrange("p (j b) -> p j b", b=HB)
+                .unsqueeze(2).to_broadcast([P, NO, NO, HB]),
+            )
+            nc.vector.tensor_copy(
+                out=c_scales[h][:].bitcast(I32).rearrange("p j (i w) -> p j i w", w=2),
+                in_=x1_scales[:, h, :].bitcast(I32).rearrange("p (j w) -> p j w", w=2)
+                .unsqueeze(2).to_broadcast([P, NO, NO, 2]),
+            )
+
+        def mx(acc, codes, scales, g, start, stop):
+            nc.tensor.matmul_mx(
+                out=acc,
+                lhsT=codes.bitcast(FP8X4),
+                lhsT_scale=scales,
+                rhs=w_codes[:, g, :].bitcast(FP8X4),
+                rhs_scale=w_scales[:, g, :],
+                start=start,
+                stop=stop,
+            )
+
+        accs = {}
+        ress = {}
+
+        def pass_p(h, j):
+            accs[(h, j)] = acc_pool.tile([P, OUT], F32, name="acc", tag="acc")
+            mx(accs[(h, j)][:], p_codes[h][:, j, :], p_scales[h][:, j, :], G_P, True, False)
+
+        def pass_c(h, j):
+            mx(accs[(h, j)][:], c_codes[h][:, j, :], c_scales[h][:, j, :], G_C, False, False)
+
+        def pass_q(h, j):
+            mx(accs[(h, j)][:], q_codes[h][:, j, :], q_scales[h][:, j, :], G_Q, False, True)
+
+        def finish(h, j):
+            jj = j % STORE_J
+            if jj == 0:
+                ress[h] = res_pool.tile([P, STORE_J, OUT], F32, name="res", tag="res")
+            res = ress[h]
+            nc.vector.tensor_tensor(out=res[:, jj, :], in0=accs[(h, j)][:], in1=aprime[h][:], op=ADD)
+            nc.scalar.activation(out=res[:, jj, :], in_=res[:, jj, :], func=SIGMOID)
+            if jj == STORE_J - 1:
+                j0 = j - jj
+                nc.sync.dma_start(
+                    out=out_v[h][:, :, j0 * OUT : (j + 1) * OUT],
+                    in_=res[:].rearrange("p j o -> p (j o)"),
+                )
+
+        x1_words = x1_sb[:].bitcast(F32)
+        transpose_pair([x1_words[:, h, :] for h in range(2)], x1_grp[:].bitcast(F32))
+        regroup_w(G_P, "v")
+        nc.vector.quantize_mx(
+            out=x1_codes[:].rearrange("p h r -> p (h r)").bitcast(FP8X4),
+            scales=x1_scales[:].rearrange("p h r -> p (h r)"),
+            in_=x1_grp[:].rearrange("p h r t -> p (h r t)"),
+        )
+        quant_w(G_P)
+
+        b2_ps = tp_pool.tile([P, OUT], F32, name="b2_ps", tag="tp")
+        nc.tensor.matmul(b2_ps[:], lhsT=ones[:], rhs=b2row[:], start=True, stop=True)
+        nc.scalar.copy(out=b2all[:], in_=b2_ps[:])
+
+        slab(0, 0)
+        c_moves(0)
+        q_moves(0, 0)
+        for j in range(0, 4):
+            pass_p(0, j)
+        regroup_w(G_C, "s")
+        quant_w(G_C)
+        slab(0, 1)
+        q_moves(0, 1)
+        for j in range(4, ACC_BUFS):
+            pass_p(0, j)
+        for j in range(ACC_BUFS):
+            pass_c(0, j)
+        slab(0, 2)
+        q_moves(0, 2)
+        regroup_w(G_Q, "v")
+        quant_w(G_Q)
+        slab(0, 3)
+        q_moves(0, 3)
+        regroup_w(G_A, "s")
+        quant_w(G_A)
+        for j in range(ACC_BUFS):
+            pass_q(0, j)
+        for h in range(2):
+            a_ps = tp_pool.tile([P, OUT], F32, name="a_ps", tag="tp")
+            mx(a_ps[:], x1_codes[:, h, :], x1_scales[:, h, :], G_A, True, True)
+            nc.vector.tensor_tensor(out=aprime[h][:], in0=a_ps[:], in1=b2all[:], op=ADD)
+        for j in range(ACC_BUFS):
+            finish(0, j)
+
+        rest = [(0, j) for j in range(ACC_BUFS, NO)] + [(1, j) for j in range(NO)]
+        for n, (h, j) in enumerate(rest):
+            if n % 2 == 0 and n // 2 < NSLAB:
+                slab(1, n // 2)
+                q_moves(1, n // 2)
+                if n == 0:
+                    c_moves(1)
+            pass_p(h, j)
+            pass_c(h, j)
+            pass_q(h, j)
+            finish(h, j)

@@ -20,12 +20,57 @@ OUT = 512
 HB = 8
 SLAB = 4
 NSLAB = NO // SLAB
-STORE_J = 4
-ACC_BUFS = 6
 
 FLOPS = 2 * NB * NO * NO * 4 * CH * OUT
 
 G_A, G_P, G_C, G_Q = 0, 1, 2, 3
+
+GROUPS = [(0, 0, 4), (0, 4, 4), (0, 8, 4), (0, 12, 4), (1, 0, 4), (1, 4, 4), (1, 8, 2), (1, 10, 2), (1, 12, 2), (1, 14, 1), (1, 15, 1)]
+
+STEPS = [
+    ("LX1",), ("LW", 1), ("LX", 0, 0), ("RW", 1, "v"), ("LB2",), ("LW", 2), ("QW", 1), ("TS", 0, 0, 0),
+    ("MB2",), ("ES", 0, 0, 0), ("LX", 0, 1), ("TS", 0, 0, 1), ("EB2",), ("ES", 0, 0, 1), ("LX", 0, 2),
+    ("TX1",), ("EX1",), ("QS", 0, 0), ("TS", 0, 1, 0), ("TS", 0, 1, 1), ("RW", 2, "s"), ("LW", 3), ("QX1",),
+    ("QMW", 0, 0, 1), ("PP", 0, 0), ("QMS", 0, 0, 1), ("CMW", 0, 0, 5), ("TS", 0, 2, 0), ("LX", 0, 3),
+    ("CMS", 0, 0, 5), ("PP", 0, 1), ("CMW", 0, 5, 16), ("PP", 0, 2), ("PP", 0, 3), ("ES", 0, 1, 0),
+    ("RW", 3, "v"), ("LW", 0), ("ES", 0, 1, 1), ("TS", 0, 2, 1), ("ES", 0, 2, 0), ("QW", 2), ("LX", 1, 0),
+    ("TS", 0, 3, 0), ("ES", 0, 2, 1), ("QS", 0, 1), ("TS", 0, 3, 1), ("PC", 0, 0), ("RW", 0, "s"), ("QW", 3),
+    ("LX", 1, 1), ("PC", 0, 1), ("PP", 0, 4), ("QMW", 0, 1, 2), ("PC", 0, 2), ("QMS", 0, 1, 2), ("PC", 0, 3),
+    ("QS", 0, 2), ("LX", 1, 2), ("PC", 0, 4), ("CMS", 0, 5, 16), ("QMW", 0, 2, 3), ("ES", 0, 3, 0),
+    ("QMS", 0, 2, 3), ("LX", 1, 3), ("QW", 0), ("ES", 0, 3, 1), ("CMW", 1, 0, 8), ("TS", 1, 0, 0),
+    ("ES", 1, 0, 0), ("PA", 0), ("QS", 0, 3), ("TS", 1, 0, 1), ("TS", 1, 1, 1), ("AA", 0), ("ES", 1, 0, 1),
+    ("QMW", 0, 3, 4), ("ES", 1, 1, 1), ("TS", 1, 1, 0), ("QMS", 0, 3, 4), ("TS", 1, 2, 0), ("QS", 1, 0),
+    ("ES", 1, 1, 0), ("PQ", 0, 0), ("CMS", 1, 0, 8), ("PQ", 0, 1), ("ES", 1, 2, 0), ("ADD", 0, 0),
+    ("PQ", 0, 2), ("PQ", 0, 3), ("ADD", 0, 1), ("SIG", 0, 0, 1), ("PQ", 0, 4), ("PP", 0, 5), ("ADD", 0, 2),
+    ("PQ", 0, 5), ("SIG", 0, 1, 1), ("PC", 0, 5), ("ADD", 0, 3), ("PP", 0, 6), ("SIG", 0, 2, 1),
+    ("PQ", 0, 6), ("PC", 0, 6), ("ADD", 0, 4), ("SIG", 0, 3, 1), ("PP", 0, 7), ("PQ", 0, 7), ("ADD", 0, 5),
+    ("SIG", 0, 4, 1), ("PC", 0, 7), ("PP", 0, 8), ("ADD", 0, 6), ("SIG", 0, 5, 1), ("PQ", 0, 8),
+    ("PC", 0, 8), ("QMW", 1, 0, 1), ("SIG", 0, 6, 1), ("TS", 1, 2, 1), ("QMS", 1, 0, 1), ("ADD", 0, 7),
+    ("PP", 0, 9), ("ES", 1, 2, 1), ("ST", 0, 0), ("PQ", 0, 9), ("QS", 1, 1), ("PC", 0, 9), ("SIG", 0, 7, 1),
+    ("PP", 0, 10), ("ADD", 0, 8), ("PQ", 0, 10), ("PC", 0, 10), ("QMW", 1, 1, 2), ("SIG", 0, 8, 1),
+    ("TS", 1, 3, 0), ("QMS", 1, 1, 2), ("ADD", 0, 9), ("TS", 1, 3, 1), ("ES", 1, 3, 0), ("PP", 0, 11),
+    ("QS", 1, 2), ("SIG", 0, 9, 1), ("PQ", 0, 11), ("ST", 0, 4), ("PC", 0, 11), ("ADD", 0, 10),
+    ("PP", 0, 12), ("ES", 1, 3, 1), ("PQ", 0, 12), ("QMW", 1, 2, 3), ("PC", 0, 12), ("SIG", 0, 10, 1),
+    ("QMS", 1, 2, 3), ("PP", 0, 13), ("CMW", 1, 8, 16), ("PQ", 0, 13), ("PC", 0, 13), ("CMS", 1, 8, 16),
+    ("PA", 1), ("ADD", 0, 11), ("PP", 0, 14), ("PQ", 0, 14), ("QS", 1, 3), ("SIG", 0, 11, 1), ("PC", 0, 14),
+    ("PP", 0, 15), ("ADD", 0, 12), ("PQ", 0, 15), ("PC", 0, 15), ("QMW", 1, 3, 4), ("SIG", 0, 12, 1),
+    ("PP", 1, 0), ("QMS", 1, 3, 4), ("PP", 1, 1), ("ADD", 0, 13), ("PQ", 1, 0), ("PC", 1, 0), ("AA", 1),
+    ("SIG", 0, 13, 1), ("PQ", 1, 1), ("ST", 0, 8), ("PC", 1, 1), ("ADD", 0, 14), ("PP", 1, 2), ("PQ", 1, 2),
+    ("ADD", 0, 15), ("PC", 1, 2), ("SIG", 0, 14, 1), ("PP", 1, 3), ("ADD", 1, 0), ("PQ", 1, 3),
+    ("SIG", 0, 15, 1), ("PC", 1, 3), ("PP", 1, 4), ("ADD", 1, 1), ("SIG", 1, 0, 1), ("PQ", 1, 4),
+    ("PC", 1, 4), ("ADD", 1, 2), ("SIG", 1, 1, 1), ("PP", 1, 5), ("PQ", 1, 5), ("ADD", 1, 3),
+    ("SIG", 1, 2, 1), ("PC", 1, 5), ("PP", 1, 6), ("ADD", 1, 4), ("PQ", 1, 6), ("SIG", 1, 3, 1),
+    ("ST", 0, 12), ("PC", 1, 6), ("ADD", 1, 5), ("PP", 1, 7), ("SIG", 1, 4, 1), ("PQ", 1, 7), ("ADD", 1, 6),
+    ("PC", 1, 7), ("SIG", 1, 5, 1), ("PP", 1, 8), ("ADD", 1, 7), ("PQ", 1, 8), ("SIG", 1, 6, 1),
+    ("PC", 1, 8), ("PP", 1, 9), ("ADD", 1, 8), ("SIG", 1, 7, 1), ("ST", 1, 0), ("PQ", 1, 9), ("PC", 1, 9),
+    ("SIG", 1, 8, 1), ("PP", 1, 10), ("ADD", 1, 9), ("PQ", 1, 10), ("PC", 1, 10), ("SIG", 1, 9, 1),
+    ("PP", 1, 11), ("ADD", 1, 10), ("PQ", 1, 11), ("PC", 1, 11), ("SIG", 1, 10, 1), ("PP", 1, 12),
+    ("ADD", 1, 11), ("ST", 1, 4), ("PQ", 1, 12), ("PC", 1, 12), ("SIG", 1, 11, 1), ("PP", 1, 13),
+    ("ADD", 1, 12), ("PQ", 1, 13), ("PC", 1, 13), ("SIG", 1, 12, 1), ("PP", 1, 14), ("ADD", 1, 13),
+    ("PQ", 1, 14), ("PC", 1, 14), ("ST", 1, 8), ("SIG", 1, 13, 1), ("PP", 1, 15), ("ADD", 1, 14),
+    ("PQ", 1, 15), ("PC", 1, 15), ("SIG", 1, 14, 1), ("ADD", 1, 15), ("ST", 1, 10), ("SIG", 1, 15, 1),
+    ("ST", 1, 12), ("ST", 1, 14), ("ST", 1, 15),
+]
 
 
 def tile_differentiablelogicmachine_pa_kernel(tc, x1, x2, W2, b2, out):
@@ -33,9 +78,10 @@ def tile_differentiablelogicmachine_pa_kernel(tc, x1, x2, W2, b2, out):
     with ExitStack() as ctx:
         keep = ctx.enter_context(tc.tile_pool(name="keep", bufs=1))
         grp_pool = ctx.enter_context(tc.tile_pool(name="grp", bufs=3))
-        res_pool = ctx.enter_context(tc.tile_pool(name="res", bufs=3))
-        tp_pool = ctx.enter_context(tc.psum_pool(name="tp", bufs=2))
-        acc_pool = ctx.enter_context(tc.psum_pool(name="acc", bufs=ACC_BUFS))
+        res_pool = ctx.enter_context(tc.tile_pool(name="res", bufs=5))
+        tp_pool = ctx.enter_context(tc.psum_pool(name="tp", bufs=3))
+        acc_pool = ctx.enter_context(tc.psum_pool(name="acc", bufs=5))
+        ctx.enter_context(tc.manual_schedule())
 
         ident = keep.tile([P, P], F32, name="ident")
         ones = keep.tile([P, P], BF16, name="ones")
@@ -67,30 +113,12 @@ def tile_differentiablelogicmachine_pa_kernel(tc, x1, x2, W2, b2, out):
         w_v = W2.rearrange("(g u p e) o -> g p u (e o)", g=4, u=2, e=2)
         out_v = out.rearrange("(h b) i j o -> h i b (j o)", h=2)
 
-        def load_w(g):
-            nc.sync.dma_start(out=w_raw[g][:].rearrange("p (u e) o -> p u (e o)", u=2), in_=w_v[g])
-
-        def load_x2(h, s):
-            nc.sync.dma_start(
-                out=x2_sb[h][s][:].rearrange("p j k -> p (j k)"),
-                in_=x2_v[h][:, :, s * SLAB * CH : (s + 1) * SLAB * CH],
-            )
+        group_of = {}
+        for h, j0, size in GROUPS:
+            for j in range(j0, j0 + size):
+                group_of[(h, j)] = (j0, size)
 
         nc.vector.memset(b2row[:], 0.0)
-        nc.scalar.dma_start(out=b2row[0:1, :], in_=b2.unsqueeze(0))
-        for h in range(2):
-            nc.sync.dma_start(out=x1_sb[:, h, :], in_=x1_v[h])
-        load_w(G_P)
-        load_x2(0, 0)
-        load_w(G_C)
-        load_x2(0, 1)
-        load_x2(0, 2)
-        load_w(G_Q)
-        load_x2(0, 3)
-        load_w(G_A)
-        for s in range(NSLAB):
-            load_x2(1, s)
-
         make_identity(nc, ident[:])
         nc.vector.memset(ones[:], 1.0)
         nc.vector.memset(warm[:], 0.0)
@@ -99,66 +127,17 @@ def tile_differentiablelogicmachine_pa_kernel(tc, x1, x2, W2, b2, out):
         for h in range(2):
             nc.vector.memset(p_scales[h][:].bitcast(I32), 0)
 
-        def regroup_w(g, engine):
-            dst = w_grp[g][:].rearrange("p (c i) t -> p c t i", i=4)
-            src = w_raw[g][:].rearrange("p t (c i) -> p c t i", i=4)
-            if engine == "v":
-                nc.vector.tensor_copy(out=dst, in_=src)
-            else:
-                nc.scalar.copy(out=dst, in_=src)
+        tps = {}
+        grps = {}
+        accs = {}
+        passes = {}
+        ress = {}
 
-        def quant_w(g):
-            nc.vector.quantize_mx(
-                out=w_codes[:, g, :].bitcast(FP8X4),
-                scales=w_scales[:, g, :],
-                in_=w_grp[g][:].rearrange("p o t -> p (o t)"),
-            )
-
-        def transpose_pair(src_words, dst_grp_words):
-            tp = tp_pool.tile([P, 2, 2, P], F32, name="tp", tag="tp")
+        def transposes(key, words):
+            tps[key] = tp_pool.tile([P, 2, 2, P], F32, name="tp", tag="tp")
             for jj in range(2):
                 for u in range(2):
-                    nc.tensor.transpose(tp[:, jj, u, :], src_words[jj][:, u * P : (u + 1) * P], ident[:])
-            nc.scalar.copy(out=dst_grp_words, in_=tp[:].rearrange("p j u r -> p j r u"))
-
-        def slab(h, s):
-            words = x2_sb[h][s][:].bitcast(F32)
-            grp = grp_pool.tile([P, SLAB, P, 4], BF16, name="x2_grp", tag="x2_grp", align_bytes=64)
-            grp_words = grp[:].bitcast(F32)
-            for half in range(SLAB // 2):
-                transpose_pair(
-                    [words[:, 2 * half + jj, :] for jj in range(2)],
-                    grp_words[:, 2 * half : 2 * half + 2, :, :],
-                )
-            lo, hi = s * SLAB, (s + 1) * SLAB
-            nc.vector.quantize_mx(
-                out=p_codes[h][:, lo:hi, :].rearrange("p j r -> p (j r)").bitcast(FP8X4),
-                scales=p_scales[h][:, lo:hi, :].rearrange("p j r -> p (j r)"),
-                in_=grp[:].rearrange("p j r t -> p (j r t)"),
-            )
-
-        def q_moves(h, s):
-            lo, hi = s * SLAB, (s + 1) * SLAB
-            nc.vector.tensor_copy(
-                out=q_codes[h][:].bitcast(I32).rearrange("p j (i b) -> p j i b", b=HB)[:, :, lo:hi, :],
-                in_=p_codes[h][:].bitcast(I32).rearrange("p i (j b) -> p j i b", b=HB)[:, :, lo:hi, :],
-            )
-            nc.vector.tensor_copy(
-                out=q_scales[h][:].bitcast(I32).rearrange("p j (i w) -> p j i w", w=2)[:, :, lo:hi, :],
-                in_=p_scales[h][:].bitcast(I32).rearrange("p i (j w) -> p j i w", w=2)[:, :, lo:hi, :],
-            )
-
-        def c_moves(h):
-            nc.vector.tensor_copy(
-                out=c_codes[h][:].bitcast(I32).rearrange("p j (i b) -> p j i b", b=HB),
-                in_=x1_codes[:, h, :].bitcast(I32).rearrange("p (j b) -> p j b", b=HB)
-                .unsqueeze(2).to_broadcast([P, NO, NO, HB]),
-            )
-            nc.vector.tensor_copy(
-                out=c_scales[h][:].bitcast(I32).rearrange("p j (i w) -> p j i w", w=2),
-                in_=x1_scales[:, h, :].bitcast(I32).rearrange("p (j w) -> p j w", w=2)
-                .unsqueeze(2).to_broadcast([P, NO, NO, 2]),
-            )
+                    nc.tensor.transpose(tps[key][:, jj, u, :], words[jj][:, u * P : (u + 1) * P], ident[:])
 
         def mx(acc, codes, scales, g, start, stop):
             nc.tensor.matmul_mx(
@@ -171,85 +150,136 @@ def tile_differentiablelogicmachine_pa_kernel(tc, x1, x2, W2, b2, out):
                 stop=stop,
             )
 
-        accs = {}
-        ress = {}
+        def tile_pass(h, j, codes, scales, g):
+            done = passes.get((h, j), 0)
+            if done == 0:
+                accs[(h, j)] = acc_pool.tile([P, OUT], F32, name="acc", tag="acc")
+            mx(accs[(h, j)][:], codes[h][:, j, :], scales[h][:, j, :], g, done == 0, done == 2)
+            passes[(h, j)] = done + 1
 
-        def pass_p(h, j):
-            accs[(h, j)] = acc_pool.tile([P, OUT], F32, name="acc", tag="acc")
-            mx(accs[(h, j)][:], p_codes[h][:, j, :], p_scales[h][:, j, :], G_P, True, False)
-
-        def pass_c(h, j):
-            mx(accs[(h, j)][:], c_codes[h][:, j, :], c_scales[h][:, j, :], G_C, False, False)
-
-        def pass_q(h, j):
-            mx(accs[(h, j)][:], q_codes[h][:, j, :], q_scales[h][:, j, :], G_Q, False, True)
-
-        def finish(h, j):
-            jj = j % STORE_J
-            if jj == 0:
-                ress[h] = res_pool.tile([P, STORE_J, OUT], F32, name="res", tag="res")
-            res = ress[h]
-            nc.vector.tensor_tensor(out=res[:, jj, :], in0=accs[(h, j)][:], in1=aprime[h][:], op=ADD)
-            nc.scalar.activation(out=res[:, jj, :], in_=res[:, jj, :], func=SIGMOID)
-            if jj == STORE_J - 1:
-                j0 = j - jj
+        for step in STEPS:
+            op = step[0]
+            if op == "LX1":
+                for h in range(2):
+                    nc.sync.dma_start(out=x1_sb[:, h, :], in_=x1_v[h])
+            elif op == "LB2":
+                nc.sync.dma_start(out=b2row[0:1, :], in_=b2.unsqueeze(0))
+            elif op == "LW":
+                g = step[1]
+                nc.sync.dma_start(out=w_raw[g][:].rearrange("p (u e) o -> p u (e o)", u=2), in_=w_v[g])
+            elif op == "LX":
+                h, s = step[1], step[2]
                 nc.sync.dma_start(
-                    out=out_v[h][:, :, j0 * OUT : (j + 1) * OUT],
-                    in_=res[:].rearrange("p j o -> p (j o)"),
+                    out=x2_sb[h][s][:].rearrange("p j k -> p (j k)"),
+                    in_=x2_v[h][:, :, s * SLAB * CH : (s + 1) * SLAB * CH],
                 )
-
-        x1_words = x1_sb[:].bitcast(F32)
-        transpose_pair([x1_words[:, h, :] for h in range(2)], x1_grp[:].bitcast(F32))
-        regroup_w(G_P, "v")
-        nc.vector.quantize_mx(
-            out=x1_codes[:].rearrange("p h r -> p (h r)").bitcast(FP8X4),
-            scales=x1_scales[:].rearrange("p h r -> p (h r)"),
-            in_=x1_grp[:].rearrange("p h r t -> p (h r t)"),
-        )
-        quant_w(G_P)
-
-        b2_ps = tp_pool.tile([P, OUT], F32, name="b2_ps", tag="tp")
-        nc.tensor.matmul(b2_ps[:], lhsT=ones[:], rhs=b2row[:], start=True, stop=True)
-        nc.scalar.copy(out=b2all[:], in_=b2_ps[:])
-
-        slab(0, 0)
-        c_moves(0)
-        q_moves(0, 0)
-        for j in range(0, 4):
-            pass_p(0, j)
-        regroup_w(G_C, "s")
-        quant_w(G_C)
-        slab(0, 1)
-        q_moves(0, 1)
-        for j in range(4, ACC_BUFS):
-            pass_p(0, j)
-        for j in range(ACC_BUFS):
-            pass_c(0, j)
-        slab(0, 2)
-        q_moves(0, 2)
-        regroup_w(G_Q, "v")
-        quant_w(G_Q)
-        slab(0, 3)
-        q_moves(0, 3)
-        regroup_w(G_A, "s")
-        quant_w(G_A)
-        for j in range(ACC_BUFS):
-            pass_q(0, j)
-        for h in range(2):
-            a_ps = tp_pool.tile([P, OUT], F32, name="a_ps", tag="tp")
-            mx(a_ps[:], x1_codes[:, h, :], x1_scales[:, h, :], G_A, True, True)
-            nc.vector.tensor_tensor(out=aprime[h][:], in0=a_ps[:], in1=b2all[:], op=ADD)
-        for j in range(ACC_BUFS):
-            finish(0, j)
-
-        rest = [(0, j) for j in range(ACC_BUFS, NO)] + [(1, j) for j in range(NO)]
-        for n, (h, j) in enumerate(rest):
-            if n % 2 == 0 and n // 2 < NSLAB:
-                slab(1, n // 2)
-                q_moves(1, n // 2)
-                if n == 0:
-                    c_moves(1)
-            pass_p(h, j)
-            pass_c(h, j)
-            pass_q(h, j)
-            finish(h, j)
+            elif op == "MB2":
+                tps["b2"] = tp_pool.tile([P, OUT], F32, name="b2_ps", tag="tp")
+                nc.tensor.matmul(tps["b2"][:], lhsT=ones[:], rhs=b2row[:], start=True, stop=True)
+            elif op == "EB2":
+                nc.scalar.copy(out=b2all[:], in_=tps["b2"][:])
+            elif op == "TX1":
+                x1_words = x1_sb[:].bitcast(F32)
+                transposes("x1", [x1_words[:, h, :] for h in range(2)])
+            elif op == "EX1":
+                nc.scalar.copy(out=x1_grp[:].bitcast(F32), in_=tps["x1"][:].rearrange("p j u r -> p j r u"))
+            elif op == "QX1":
+                nc.vector.quantize_mx(
+                    out=x1_codes[:].rearrange("p h r -> p (h r)").bitcast(FP8X4),
+                    scales=x1_scales[:].rearrange("p h r -> p (h r)"),
+                    in_=x1_grp[:].rearrange("p h r t -> p (h r t)"),
+                )
+            elif op == "RW":
+                g = step[1]
+                dst = w_grp[g][:].rearrange("p (c i) t -> p c t i", i=4)
+                src = w_raw[g][:].rearrange("p t (c i) -> p c t i", i=4)
+                if step[2] == "v":
+                    nc.vector.tensor_copy(out=dst, in_=src)
+                else:
+                    nc.scalar.copy(out=dst, in_=src)
+            elif op == "QW":
+                g = step[1]
+                nc.vector.quantize_mx(
+                    out=w_codes[:, g, :].bitcast(FP8X4),
+                    scales=w_scales[:, g, :],
+                    in_=w_grp[g][:].rearrange("p o t -> p (o t)"),
+                )
+            elif op == "TS":
+                h, s, half = step[1], step[2], step[3]
+                words = x2_sb[h][s][:].bitcast(F32)
+                transposes((h, s, half), [words[:, 2 * half + jj, :] for jj in range(2)])
+            elif op == "ES":
+                h, s, half = step[1], step[2], step[3]
+                if (h, s) not in grps:
+                    grps[(h, s)] = grp_pool.tile([P, SLAB, P, 4], BF16, name="x2_grp", tag="x2_grp", align_bytes=64)
+                nc.scalar.copy(
+                    out=grps[(h, s)][:].bitcast(F32)[:, 2 * half : 2 * half + 2, :, :],
+                    in_=tps[(h, s, half)][:].rearrange("p j u r -> p j r u"),
+                )
+            elif op == "QS":
+                h, s = step[1], step[2]
+                lo, hi = s * SLAB, (s + 1) * SLAB
+                nc.vector.quantize_mx(
+                    out=p_codes[h][:, lo:hi, :].rearrange("p j r -> p (j r)").bitcast(FP8X4),
+                    scales=p_scales[h][:, lo:hi, :].rearrange("p j r -> p (j r)"),
+                    in_=grps[(h, s)][:].rearrange("p j r t -> p (j r t)"),
+                )
+            elif op == "QMW":
+                h, lo, hi = step[1], step[2] * SLAB, step[3] * SLAB
+                nc.vector.tensor_copy(
+                    out=q_codes[h][:].bitcast(I32).rearrange("p j (i b) -> p j i b", b=HB)[:, :, lo:hi, :],
+                    in_=p_codes[h][:].bitcast(I32).rearrange("p i (j b) -> p j i b", b=HB)[:, :, lo:hi, :],
+                )
+            elif op == "QMS":
+                h, lo, hi = step[1], step[2] * SLAB, step[3] * SLAB
+                nc.vector.tensor_copy(
+                    out=q_scales[h][:].bitcast(I32).rearrange("p j (i w) -> p j i w", w=2)[:, :, lo:hi, :],
+                    in_=p_scales[h][:].bitcast(I32).rearrange("p i (j w) -> p j i w", w=2)[:, :, lo:hi, :],
+                )
+            elif op == "CMW":
+                h, lo, hi = step[1], step[2], step[3]
+                nc.vector.tensor_copy(
+                    out=c_codes[h][:, lo:hi, :].bitcast(I32).rearrange("p j (i b) -> p j i b", b=HB),
+                    in_=x1_codes[:, h, lo * HB : hi * HB].bitcast(I32).rearrange("p (j b) -> p j b", b=HB)
+                    .unsqueeze(2).to_broadcast([P, hi - lo, NO, HB]),
+                )
+            elif op == "CMS":
+                h, lo, hi = step[1], step[2], step[3]
+                nc.vector.tensor_copy(
+                    out=c_scales[h][:, lo:hi, :].bitcast(I32).rearrange("p j (i w) -> p j i w", w=2),
+                    in_=x1_scales[:, h, lo * HB : hi * HB].bitcast(I32).rearrange("p (j w) -> p j w", w=2)
+                    .unsqueeze(2).to_broadcast([P, hi - lo, NO, 2]),
+                )
+            elif op == "PP":
+                tile_pass(step[1], step[2], p_codes, p_scales, G_P)
+            elif op == "PC":
+                tile_pass(step[1], step[2], c_codes, c_scales, G_C)
+            elif op == "PQ":
+                tile_pass(step[1], step[2], q_codes, q_scales, G_Q)
+            elif op == "PA":
+                h = step[1]
+                tps[("a", h)] = tp_pool.tile([P, OUT], F32, name="a_ps", tag="tp")
+                mx(tps[("a", h)][:], x1_codes[:, h, :], x1_scales[:, h, :], G_A, True, True)
+            elif op == "AA":
+                h = step[1]
+                nc.vector.tensor_tensor(out=aprime[h][:], in0=tps[("a", h)][:], in1=b2all[:], op=ADD)
+            elif op == "ADD":
+                h, j = step[1], step[2]
+                j0, size = group_of[(h, j)]
+                if j == j0:
+                    ress[(h, j0)] = res_pool.tile([P, size, OUT], F32, name="res", tag="res")
+                nc.vector.tensor_tensor(out=ress[(h, j0)][:, j - j0, :], in0=accs[(h, j)][:], in1=aprime[h][:], op=ADD)
+            elif op == "SIG":
+                h, j, n = step[1], step[2], step[3]
+                j0, size = group_of[(h, j)]
+                part = ress[(h, j0)][:, j - j0 : j - j0 + n, :]
+                nc.scalar.activation(out=part, in_=part, func=SIGMOID)
+            elif op == "ST":
+                h, j0 = step[1], step[2]
+                size = group_of[(h, j0)][1]
+                nc.sync.dma_start(
+                    out=out_v[h][:, :, j0 * OUT : (j0 + size) * OUT],
+                    in_=ress[(h, j0)][:].rearrange("p j o -> p (j o)"),
+                )
+            else:
+                raise ValueError(op)

@@ -28,47 +28,46 @@ G_A, G_P, G_C, G_Q = 0, 1, 2, 3
 GROUPS = [(0, 0, 4), (0, 4, 4), (0, 8, 4), (0, 12, 4), (1, 0, 4), (1, 4, 4), (1, 8, 2), (1, 10, 2), (1, 12, 2), (1, 14, 1), (1, 15, 1)]
 
 STEPS = [
-    ("LX1",), ("LW", 1), ("LX", 0, 0), ("RW", 1, "v"), ("LB2",), ("LW", 2), ("QW", 1), ("TS", 0, 0, 0),
-    ("MB2",), ("ES", 0, 0, 0), ("LX", 0, 1), ("TS", 0, 0, 1), ("EB2",), ("ES", 0, 0, 1), ("LX", 0, 2),
-    ("TX1",), ("EX1",), ("QS", 0, 0), ("TS", 0, 1, 0), ("TS", 0, 1, 1), ("RW", 2, "s"), ("LW", 3), ("QX1",),
-    ("QMW", 0, 0, 1), ("PP", 0, 0), ("QMS", 0, 0, 1), ("CMW", 0, 0, 5), ("TS", 0, 2, 0), ("LX", 0, 3),
-    ("CMS", 0, 0, 5), ("PP", 0, 1), ("CMW", 0, 5, 16), ("PP", 0, 2), ("PP", 0, 3), ("ES", 0, 1, 0),
-    ("RW", 3, "v"), ("LW", 0), ("ES", 0, 1, 1), ("TS", 0, 2, 1), ("ES", 0, 2, 0), ("QW", 2), ("LX", 1, 0),
-    ("TS", 0, 3, 0), ("ES", 0, 2, 1), ("QS", 0, 1), ("TS", 0, 3, 1), ("PC", 0, 0), ("RW", 0, "s"), ("QW", 3),
-    ("LX", 1, 1), ("PC", 0, 1), ("PP", 0, 4), ("QMW", 0, 1, 2), ("PC", 0, 2), ("QMS", 0, 1, 2), ("PC", 0, 3),
-    ("QS", 0, 2), ("LX", 1, 2), ("PC", 0, 4), ("CMS", 0, 5, 16), ("QMW", 0, 2, 3), ("ES", 0, 3, 0),
-    ("QMS", 0, 2, 3), ("LX", 1, 3), ("QW", 0), ("ES", 0, 3, 1), ("CMW", 1, 0, 8), ("TS", 1, 0, 0),
-    ("ES", 1, 0, 0), ("PA", 0), ("QS", 0, 3), ("TS", 1, 0, 1), ("TS", 1, 1, 1), ("AA", 0), ("ES", 1, 0, 1),
-    ("QMW", 0, 3, 4), ("ES", 1, 1, 1), ("TS", 1, 1, 0), ("QMS", 0, 3, 4), ("TS", 1, 2, 0), ("QS", 1, 0),
-    ("ES", 1, 1, 0), ("PQ", 0, 0), ("CMS", 1, 0, 8), ("PQ", 0, 1), ("ES", 1, 2, 0), ("ADD", 0, 0),
-    ("PQ", 0, 2), ("PQ", 0, 3), ("ADD", 0, 1), ("SIG", 0, 0, 1), ("PQ", 0, 4), ("PP", 0, 5), ("ADD", 0, 2),
-    ("PQ", 0, 5), ("SIG", 0, 1, 1), ("PC", 0, 5), ("ADD", 0, 3), ("PP", 0, 6), ("SIG", 0, 2, 1),
-    ("PQ", 0, 6), ("PC", 0, 6), ("ADD", 0, 4), ("SIG", 0, 3, 1), ("PP", 0, 7), ("PQ", 0, 7), ("ADD", 0, 5),
-    ("SIG", 0, 4, 1), ("PC", 0, 7), ("PP", 0, 8), ("ADD", 0, 6), ("SIG", 0, 5, 1), ("PQ", 0, 8),
-    ("PC", 0, 8), ("QMW", 1, 0, 1), ("SIG", 0, 6, 1), ("TS", 1, 2, 1), ("QMS", 1, 0, 1), ("ADD", 0, 7),
-    ("PP", 0, 9), ("ES", 1, 2, 1), ("ST", 0, 0), ("PQ", 0, 9), ("QS", 1, 1), ("PC", 0, 9), ("SIG", 0, 7, 1),
-    ("PP", 0, 10), ("ADD", 0, 8), ("PQ", 0, 10), ("PC", 0, 10), ("QMW", 1, 1, 2), ("SIG", 0, 8, 1),
-    ("TS", 1, 3, 0), ("QMS", 1, 1, 2), ("ADD", 0, 9), ("TS", 1, 3, 1), ("ES", 1, 3, 0), ("PP", 0, 11),
-    ("QS", 1, 2), ("SIG", 0, 9, 1), ("PQ", 0, 11), ("ST", 0, 4), ("PC", 0, 11), ("ADD", 0, 10),
-    ("PP", 0, 12), ("ES", 1, 3, 1), ("PQ", 0, 12), ("QMW", 1, 2, 3), ("PC", 0, 12), ("SIG", 0, 10, 1),
-    ("QMS", 1, 2, 3), ("PP", 0, 13), ("CMW", 1, 8, 16), ("PQ", 0, 13), ("PC", 0, 13), ("CMS", 1, 8, 16),
-    ("PA", 1), ("ADD", 0, 11), ("PP", 0, 14), ("PQ", 0, 14), ("QS", 1, 3), ("SIG", 0, 11, 1), ("PC", 0, 14),
-    ("PP", 0, 15), ("ADD", 0, 12), ("PQ", 0, 15), ("PC", 0, 15), ("QMW", 1, 3, 4), ("SIG", 0, 12, 1),
-    ("PP", 1, 0), ("QMS", 1, 3, 4), ("PP", 1, 1), ("ADD", 0, 13), ("PQ", 1, 0), ("PC", 1, 0), ("AA", 1),
-    ("SIG", 0, 13, 1), ("PQ", 1, 1), ("ST", 0, 8), ("PC", 1, 1), ("ADD", 0, 14), ("PP", 1, 2), ("PQ", 1, 2),
-    ("ADD", 0, 15), ("PC", 1, 2), ("SIG", 0, 14, 1), ("PP", 1, 3), ("ADD", 1, 0), ("PQ", 1, 3),
-    ("SIG", 0, 15, 1), ("PC", 1, 3), ("PP", 1, 4), ("ADD", 1, 1), ("SIG", 1, 0, 1), ("PQ", 1, 4),
-    ("PC", 1, 4), ("ADD", 1, 2), ("SIG", 1, 1, 1), ("PP", 1, 5), ("PQ", 1, 5), ("ADD", 1, 3),
-    ("SIG", 1, 2, 1), ("PC", 1, 5), ("PP", 1, 6), ("ADD", 1, 4), ("PQ", 1, 6), ("SIG", 1, 3, 1),
-    ("ST", 0, 12), ("PC", 1, 6), ("ADD", 1, 5), ("PP", 1, 7), ("SIG", 1, 4, 1), ("PQ", 1, 7), ("ADD", 1, 6),
-    ("PC", 1, 7), ("SIG", 1, 5, 1), ("PP", 1, 8), ("ADD", 1, 7), ("PQ", 1, 8), ("SIG", 1, 6, 1),
-    ("PC", 1, 8), ("PP", 1, 9), ("ADD", 1, 8), ("SIG", 1, 7, 1), ("ST", 1, 0), ("PQ", 1, 9), ("PC", 1, 9),
-    ("SIG", 1, 8, 1), ("PP", 1, 10), ("ADD", 1, 9), ("PQ", 1, 10), ("PC", 1, 10), ("SIG", 1, 9, 1),
-    ("PP", 1, 11), ("ADD", 1, 10), ("PQ", 1, 11), ("PC", 1, 11), ("SIG", 1, 10, 1), ("PP", 1, 12),
-    ("ADD", 1, 11), ("ST", 1, 4), ("PQ", 1, 12), ("PC", 1, 12), ("SIG", 1, 11, 1), ("PP", 1, 13),
-    ("ADD", 1, 12), ("PQ", 1, 13), ("PC", 1, 13), ("SIG", 1, 12, 1), ("PP", 1, 14), ("ADD", 1, 13),
-    ("PQ", 1, 14), ("PC", 1, 14), ("ST", 1, 8), ("SIG", 1, 13, 1), ("PP", 1, 15), ("ADD", 1, 14),
-    ("PQ", 1, 15), ("PC", 1, 15), ("SIG", 1, 14, 1), ("ADD", 1, 15), ("ST", 1, 10), ("SIG", 1, 15, 1),
+    ("LX1",), ("LW", 1), ("LX", 0, 0), ("TX1",), ("LB2",), ("LW", 2), ("RW", 1, "v"), ("EX1",), ("LX", 0, 1),
+    ("TS", 0, 0, 0), ("QX1",), ("TS", 0, 0, 1), ("QW", 1), ("CMW", 1, 4, 16), ("LX", 0, 2), ("RW", 2, "s"),
+    ("CMW", 1, 0, 4), ("LW", 3), ("CMW", 0, 5, 16), ("TS", 0, 1, 0), ("CMS", 0, 5, 16), ("CMW", 0, 0, 5),
+    ("LX", 0, 3), ("ES", 0, 0, 0), ("QW", 2), ("ES", 0, 0, 1), ("LW", 0), ("TS", 0, 1, 1), ("RW", 3, "v"),
+    ("ES", 0, 1, 0), ("TS", 0, 2, 0), ("LX", 1, 0), ("TS", 0, 2, 1), ("ES", 0, 1, 1), ("QS", 0, 0),
+    ("ES", 0, 2, 0), ("QW", 3), ("TS", 0, 3, 0), ("LX", 1, 1), ("ES", 0, 2, 1), ("CMS", 0, 0, 5),
+    ("PP", 0, 0), ("RW", 0, "v"), ("TS", 0, 3, 1), ("LX", 1, 2), ("ES", 0, 3, 0), ("MB2",), ("PP", 0, 1),
+    ("QS", 0, 1), ("PC", 0, 1), ("ES", 0, 3, 1), ("PC", 0, 0), ("LX", 1, 3), ("QW", 0), ("PP", 0, 2),
+    ("EB2",), ("PP", 0, 3), ("QS", 0, 2), ("PP", 0, 4), ("PC", 0, 4), ("QS", 0, 3), ("PA", 0), ("PC", 0, 3),
+    ("CMS", 1, 4, 16), ("TS", 1, 0, 0), ("QMW", 0, 0, 5), ("TS", 1, 0, 1), ("QMS", 0, 0, 5), ("AA", 0),
+    ("PC", 0, 2), ("PQ", 0, 0), ("ES", 1, 0, 0), ("QMS", 0, 5, 16), ("PQ", 0, 1), ("QMW", 0, 5, 16),
+    ("PQ", 0, 3), ("ES", 1, 0, 1), ("PQ", 0, 2), ("PQ", 0, 4), ("ADD", 0, 0), ("TS", 1, 1, 0), ("ADD", 0, 1),
+    ("TS", 1, 1, 1), ("TS", 1, 2, 0), ("QS", 1, 0), ("ES", 1, 1, 0), ("PP", 0, 5), ("PP", 0, 6),
+    ("ADD", 0, 2), ("ES", 1, 1, 1), ("PQ", 0, 5), ("PC", 0, 5), ("ADD", 0, 3), ("ES", 1, 2, 0), ("PQ", 0, 6),
+    ("PC", 0, 6), ("CMS", 1, 0, 4), ("ADD", 0, 4), ("TS", 1, 2, 1), ("TS", 1, 3, 0), ("QS", 1, 1),
+    ("TS", 1, 3, 1), ("ADD", 0, 5), ("ES", 1, 2, 1), ("PP", 0, 7), ("PP", 0, 8), ("ADD", 0, 6),
+    ("ES", 1, 3, 0), ("PP", 0, 9), ("PQ", 0, 7), ("QS", 1, 2), ("SIG", 0, 2, 1), ("PC", 0, 7), ("PQ", 0, 8),
+    ("ES", 1, 3, 1), ("PP", 0, 10), ("PC", 0, 8), ("ADD", 0, 7), ("SIG", 0, 3, 1), ("PQ", 0, 9),
+    ("PC", 0, 9), ("SIG", 0, 4, 1), ("PQ", 0, 10), ("QS", 1, 3), ("PC", 0, 10), ("SIG", 0, 0, 1),
+    ("PP", 0, 11), ("ADD", 0, 8), ("PQ", 0, 11), ("SIG", 0, 1, 1), ("PP", 0, 12), ("ADD", 0, 9),
+    ("PC", 0, 11), ("SIG", 0, 7, 1), ("PQ", 0, 12), ("ADD", 0, 10), ("PA", 1), ("SIG", 0, 8, 1),
+    ("PP", 0, 13), ("QMS", 1, 0, 4), ("PC", 0, 12), ("ADD", 0, 11), ("SIG", 0, 5, 1), ("PQ", 0, 13),
+    ("PC", 0, 13), ("QMW", 1, 0, 4), ("SIG", 0, 6, 1), ("PP", 0, 14), ("ADD", 0, 12), ("PQ", 0, 14),
+    ("SIG", 0, 10, 1), ("PP", 0, 15), ("PP", 1, 0), ("ADD", 0, 13), ("SIG", 0, 11, 1), ("PC", 0, 14),
+    ("PQ", 0, 15), ("AA", 1), ("SIG", 0, 12, 1), ("PC", 0, 15), ("ST", 0, 0), ("PP", 1, 1),
+    ("SIG", 0, 13, 1), ("ADD", 0, 14), ("PP", 1, 2), ("PQ", 1, 0), ("SIG", 0, 9, 1), ("PQ", 1, 2),
+    ("ADD", 0, 15), ("PC", 1, 0), ("SIG", 0, 14, 1), ("PQ", 1, 1), ("QMW", 1, 4, 16), ("PC", 1, 2),
+    ("SIG", 0, 15, 1), ("PP", 1, 3), ("ST", 0, 4), ("PC", 1, 1), ("QMS", 1, 4, 16), ("PQ", 1, 3),
+    ("ADD", 1, 0), ("PC", 1, 3), ("PP", 1, 4), ("ADD", 1, 1), ("PQ", 1, 4), ("PC", 1, 4), ("SIG", 1, 0, 1),
+    ("PP", 1, 5), ("ADD", 1, 2), ("PQ", 1, 5), ("SIG", 1, 1, 1), ("PC", 1, 5), ("ADD", 1, 3), ("PP", 1, 6),
+    ("ST", 0, 8), ("SIG", 1, 2, 1), ("PQ", 1, 6), ("ADD", 1, 4), ("PC", 1, 6), ("SIG", 1, 3, 1),
+    ("PP", 1, 7), ("ADD", 1, 5), ("PQ", 1, 7), ("PC", 1, 7), ("SIG", 1, 4, 1), ("ADD", 1, 6), ("PP", 1, 8),
+    ("PQ", 1, 8), ("SIG", 1, 5, 1), ("PC", 1, 8), ("ST", 0, 12), ("ADD", 1, 7), ("PP", 1, 9),
+    ("SIG", 1, 6, 1), ("PP", 1, 10), ("PQ", 1, 9), ("ADD", 1, 8), ("PC", 1, 9), ("SIG", 1, 7, 1),
+    ("PQ", 1, 10), ("PP", 1, 11), ("PC", 1, 10), ("SIG", 1, 8, 1), ("ADD", 1, 9), ("PQ", 1, 11),
+    ("PP", 1, 12), ("ST", 1, 0), ("PC", 1, 11), ("ADD", 1, 10), ("PQ", 1, 12), ("SIG", 1, 9, 1),
+    ("PC", 1, 12), ("PP", 1, 13), ("ADD", 1, 11), ("PQ", 1, 13), ("SIG", 1, 10, 1), ("PC", 1, 13),
+    ("PP", 1, 14), ("ADD", 1, 12), ("PQ", 1, 14), ("SIG", 1, 11, 1), ("PC", 1, 14), ("ADD", 1, 13),
+    ("ST", 1, 4), ("PP", 1, 15), ("SIG", 1, 12, 1), ("PQ", 1, 15), ("PC", 1, 15), ("ADD", 1, 14),
+    ("SIG", 1, 13, 1), ("ADD", 1, 15), ("SIG", 1, 14, 1), ("ST", 1, 8), ("SIG", 1, 15, 1), ("ST", 1, 10),
     ("ST", 1, 12), ("ST", 1, 14), ("ST", 1, 15),
 ]
 
@@ -77,8 +76,12 @@ def tile_differentiablelogicmachine_pa_kernel(tc, x1, x2, W2, b2, out):
     nc = tc.nc
     with ExitStack() as ctx:
         keep = ctx.enter_context(tc.tile_pool(name="keep", bufs=1))
-        grp_pool = ctx.enter_context(tc.tile_pool(name="grp", bufs=3))
-        res_pool = ctx.enter_context(tc.tile_pool(name="res", bufs=5))
+        grp_pool = ctx.enter_context(tc.tile_pool(name="grp", bufs=5))
+        res_pools = {
+            4: ctx.enter_context(tc.tile_pool(name="res4", bufs=5)),
+            2: ctx.enter_context(tc.tile_pool(name="res2", bufs=3)),
+            1: ctx.enter_context(tc.tile_pool(name="res1", bufs=2)),
+        }
         tp_pool = ctx.enter_context(tc.psum_pool(name="tp", bufs=3))
         acc_pool = ctx.enter_context(tc.psum_pool(name="acc", bufs=5))
         ctx.enter_context(tc.manual_schedule())
@@ -225,16 +228,16 @@ def tile_differentiablelogicmachine_pa_kernel(tc, x1, x2, W2, b2, out):
                     in_=grps[(h, s)][:].rearrange("p j r t -> p (j r t)"),
                 )
             elif op == "QMW":
-                h, lo, hi = step[1], step[2] * SLAB, step[3] * SLAB
+                h, lo, hi = step[1], step[2], step[3]
                 nc.vector.tensor_copy(
-                    out=q_codes[h][:].bitcast(I32).rearrange("p j (i b) -> p j i b", b=HB)[:, :, lo:hi, :],
-                    in_=p_codes[h][:].bitcast(I32).rearrange("p i (j b) -> p j i b", b=HB)[:, :, lo:hi, :],
+                    out=q_codes[h][:, lo:hi, :].bitcast(I32).rearrange("p j (i b) -> p j i b", b=HB),
+                    in_=p_codes[h][:].bitcast(I32).rearrange("p i (j b) -> p j i b", b=HB)[:, lo:hi, :, :],
                 )
             elif op == "QMS":
-                h, lo, hi = step[1], step[2] * SLAB, step[3] * SLAB
+                h, lo, hi = step[1], step[2], step[3]
                 nc.vector.tensor_copy(
-                    out=q_scales[h][:].bitcast(I32).rearrange("p j (i w) -> p j i w", w=2)[:, :, lo:hi, :],
-                    in_=p_scales[h][:].bitcast(I32).rearrange("p i (j w) -> p j i w", w=2)[:, :, lo:hi, :],
+                    out=q_scales[h][:, lo:hi, :].bitcast(I32).rearrange("p j (i w) -> p j i w", w=2),
+                    in_=p_scales[h][:].bitcast(I32).rearrange("p i (j w) -> p j i w", w=2)[:, lo:hi, :, :],
                 )
             elif op == "CMW":
                 h, lo, hi = step[1], step[2], step[3]
@@ -267,7 +270,7 @@ def tile_differentiablelogicmachine_pa_kernel(tc, x1, x2, W2, b2, out):
                 h, j = step[1], step[2]
                 j0, size = group_of[(h, j)]
                 if j == j0:
-                    ress[(h, j0)] = res_pool.tile([P, size, OUT], F32, name="res", tag="res")
+                    ress[(h, j0)] = res_pools[size].tile([P, size, OUT], F32, name="res", tag="res")
                 nc.vector.tensor_tensor(out=ress[(h, j0)][:, j - j0, :], in0=accs[(h, j)][:], in1=aprime[h][:], op=ADD)
             elif op == "SIG":
                 h, j, n = step[1], step[2], step[3]

@@ -28,47 +28,49 @@ G_A, G_P, G_C, G_Q = 0, 1, 2, 3
 GROUPS = [(0, 0, 4), (0, 4, 4), (0, 8, 4), (0, 12, 4), (1, 0, 4), (1, 4, 4), (1, 8, 2), (1, 10, 2), (1, 12, 2), (1, 14, 1), (1, 15, 1)]
 
 STEPS = [
-    ("LX1",), ("LW", 1), ("LX", 0, 0), ("TX1",), ("LB2",), ("LW", 2), ("RW", 1, "v"), ("EX1",), ("LX", 0, 1),
-    ("TS", 0, 0, 0), ("QX1",), ("TS", 0, 0, 1), ("QW", 1), ("CMW", 1, 4, 16), ("LX", 0, 2), ("RW", 2, "s"),
-    ("CMW", 1, 0, 4), ("LW", 3), ("CMW", 0, 5, 16), ("TS", 0, 1, 0), ("CMS", 0, 5, 16), ("CMW", 0, 0, 5),
-    ("LX", 0, 3), ("ES", 0, 0, 0), ("QW", 2), ("ES", 0, 0, 1), ("LW", 0), ("TS", 0, 1, 1), ("RW", 3, "v"),
-    ("ES", 0, 1, 0), ("TS", 0, 2, 0), ("LX", 1, 0), ("TS", 0, 2, 1), ("ES", 0, 1, 1), ("QS", 0, 0),
-    ("ES", 0, 2, 0), ("QW", 3), ("TS", 0, 3, 0), ("LX", 1, 1), ("ES", 0, 2, 1), ("CMS", 0, 0, 5),
-    ("PP", 0, 0), ("RW", 0, "v"), ("TS", 0, 3, 1), ("LX", 1, 2), ("ES", 0, 3, 0), ("MB2",), ("PP", 0, 1),
-    ("QS", 0, 1), ("PC", 0, 1), ("ES", 0, 3, 1), ("PC", 0, 0), ("LX", 1, 3), ("QW", 0), ("PP", 0, 2),
-    ("EB2",), ("PP", 0, 3), ("QS", 0, 2), ("PP", 0, 4), ("PC", 0, 4), ("QS", 0, 3), ("PA", 0), ("PC", 0, 3),
-    ("CMS", 1, 4, 16), ("TS", 1, 0, 0), ("QMW", 0, 0, 5), ("TS", 1, 0, 1), ("QMS", 0, 0, 5), ("AA", 0),
-    ("PC", 0, 2), ("PQ", 0, 0), ("ES", 1, 0, 0), ("QMS", 0, 5, 16), ("PQ", 0, 1), ("QMW", 0, 5, 16),
-    ("PQ", 0, 3), ("ES", 1, 0, 1), ("PQ", 0, 2), ("PQ", 0, 4), ("ADD", 0, 0), ("TS", 1, 1, 0), ("ADD", 0, 1),
-    ("TS", 1, 1, 1), ("TS", 1, 2, 0), ("QS", 1, 0), ("ES", 1, 1, 0), ("PP", 0, 5), ("PP", 0, 6),
-    ("ADD", 0, 2), ("ES", 1, 1, 1), ("PQ", 0, 5), ("PC", 0, 5), ("ADD", 0, 3), ("ES", 1, 2, 0), ("PQ", 0, 6),
-    ("PC", 0, 6), ("CMS", 1, 0, 4), ("ADD", 0, 4), ("TS", 1, 2, 1), ("TS", 1, 3, 0), ("QS", 1, 1),
-    ("TS", 1, 3, 1), ("ADD", 0, 5), ("ES", 1, 2, 1), ("PP", 0, 7), ("PP", 0, 8), ("ADD", 0, 6),
-    ("ES", 1, 3, 0), ("PP", 0, 9), ("PQ", 0, 7), ("QS", 1, 2), ("SIG", 0, 2, 1), ("PC", 0, 7), ("PQ", 0, 8),
-    ("ES", 1, 3, 1), ("PP", 0, 10), ("PC", 0, 8), ("ADD", 0, 7), ("SIG", 0, 3, 1), ("PQ", 0, 9),
-    ("PC", 0, 9), ("SIG", 0, 4, 1), ("PQ", 0, 10), ("QS", 1, 3), ("PC", 0, 10), ("SIG", 0, 0, 1),
-    ("PP", 0, 11), ("ADD", 0, 8), ("PQ", 0, 11), ("SIG", 0, 1, 1), ("PP", 0, 12), ("ADD", 0, 9),
-    ("PC", 0, 11), ("SIG", 0, 7, 1), ("PQ", 0, 12), ("ADD", 0, 10), ("PA", 1), ("SIG", 0, 8, 1),
-    ("PP", 0, 13), ("QMS", 1, 0, 4), ("PC", 0, 12), ("ADD", 0, 11), ("SIG", 0, 5, 1), ("PQ", 0, 13),
-    ("PC", 0, 13), ("QMW", 1, 0, 4), ("SIG", 0, 6, 1), ("PP", 0, 14), ("ADD", 0, 12), ("PQ", 0, 14),
-    ("SIG", 0, 10, 1), ("PP", 0, 15), ("PP", 1, 0), ("ADD", 0, 13), ("SIG", 0, 11, 1), ("PC", 0, 14),
-    ("PQ", 0, 15), ("AA", 1), ("SIG", 0, 12, 1), ("PC", 0, 15), ("ST", 0, 0), ("PP", 1, 1),
-    ("SIG", 0, 13, 1), ("ADD", 0, 14), ("PP", 1, 2), ("PQ", 1, 0), ("SIG", 0, 9, 1), ("PQ", 1, 2),
-    ("ADD", 0, 15), ("PC", 1, 0), ("SIG", 0, 14, 1), ("PQ", 1, 1), ("QMW", 1, 4, 16), ("PC", 1, 2),
-    ("SIG", 0, 15, 1), ("PP", 1, 3), ("ST", 0, 4), ("PC", 1, 1), ("QMS", 1, 4, 16), ("PQ", 1, 3),
-    ("ADD", 1, 0), ("PC", 1, 3), ("PP", 1, 4), ("ADD", 1, 1), ("PQ", 1, 4), ("PC", 1, 4), ("SIG", 1, 0, 1),
-    ("PP", 1, 5), ("ADD", 1, 2), ("PQ", 1, 5), ("SIG", 1, 1, 1), ("PC", 1, 5), ("ADD", 1, 3), ("PP", 1, 6),
-    ("ST", 0, 8), ("SIG", 1, 2, 1), ("PQ", 1, 6), ("ADD", 1, 4), ("PC", 1, 6), ("SIG", 1, 3, 1),
-    ("PP", 1, 7), ("ADD", 1, 5), ("PQ", 1, 7), ("PC", 1, 7), ("SIG", 1, 4, 1), ("ADD", 1, 6), ("PP", 1, 8),
-    ("PQ", 1, 8), ("SIG", 1, 5, 1), ("PC", 1, 8), ("ST", 0, 12), ("ADD", 1, 7), ("PP", 1, 9),
-    ("SIG", 1, 6, 1), ("PP", 1, 10), ("PQ", 1, 9), ("ADD", 1, 8), ("PC", 1, 9), ("SIG", 1, 7, 1),
-    ("PQ", 1, 10), ("PP", 1, 11), ("PC", 1, 10), ("SIG", 1, 8, 1), ("ADD", 1, 9), ("PQ", 1, 11),
-    ("PP", 1, 12), ("ST", 1, 0), ("PC", 1, 11), ("ADD", 1, 10), ("PQ", 1, 12), ("SIG", 1, 9, 1),
-    ("PC", 1, 12), ("PP", 1, 13), ("ADD", 1, 11), ("PQ", 1, 13), ("SIG", 1, 10, 1), ("PC", 1, 13),
-    ("PP", 1, 14), ("ADD", 1, 12), ("PQ", 1, 14), ("SIG", 1, 11, 1), ("PC", 1, 14), ("ADD", 1, 13),
-    ("ST", 1, 4), ("PP", 1, 15), ("SIG", 1, 12, 1), ("PQ", 1, 15), ("PC", 1, 15), ("ADD", 1, 14),
-    ("SIG", 1, 13, 1), ("ADD", 1, 15), ("SIG", 1, 14, 1), ("ST", 1, 8), ("SIG", 1, 15, 1), ("ST", 1, 10),
-    ("ST", 1, 12), ("ST", 1, 14), ("ST", 1, 15),
+    ("LX1",), ("LW", 1), ("TX1",), ("LX", 0, 0), ("EX1",), ("RW", 1, "v"), ("LB2",), ("LW", 2),
+    ("TS", 0, 0, 0), ("LX", 0, 1), ("QX1",), ("TS", 0, 0, 1), ("QW", 1), ("ES", 0, 0, 0), ("CMW", 0, 0, 5),
+    ("LX", 0, 2), ("CMS", 0, 0, 5), ("ES", 0, 0, 1), ("CMW", 0, 5, 16), ("RW", 2, "s"), ("TS", 0, 1, 0),
+    ("LW", 3), ("QS", 0, 0), ("TS", 0, 1, 1), ("CMS", 0, 5, 16), ("CMS", 1, 0, 4), ("CMW", 1, 0, 4),
+    ("PP", 0, 0), ("LX", 0, 3), ("CMW", 1, 4, 16), ("TS", 0, 2, 0), ("PP", 0, 1), ("RW", 3, "v"),
+    ("ES", 0, 1, 0), ("LW", 0), ("PP", 0, 2), ("PP", 0, 3), ("ES", 0, 1, 1), ("TS", 0, 2, 1),
+    ("ES", 0, 2, 0), ("LX", 1, 0), ("QW", 2), ("TS", 0, 3, 0), ("QS", 0, 1), ("ES", 0, 2, 1),
+    ("TS", 0, 3, 1), ("LX", 1, 1), ("PC", 0, 0), ("RW", 0, "v"), ("ES", 0, 3, 0), ("PC", 0, 1),
+    ("ES", 0, 3, 1), ("MB2",), ("LX", 1, 2), ("PP", 0, 4), ("PC", 0, 2), ("QW", 0), ("EB2",),
+    ("TS", 1, 0, 0), ("QS", 0, 2), ("LX", 1, 3), ("PC", 0, 3), ("PC", 0, 4), ("QW", 3), ("ES", 1, 0, 0),
+    ("PA", 0), ("QS", 0, 3), ("TS", 1, 0, 1), ("TS", 1, 1, 1), ("CMS", 1, 4, 16), ("QMW", 0, 0, 5),
+    ("ES", 1, 0, 1), ("QMS", 0, 0, 5), ("AA", 0), ("ES", 1, 1, 1), ("PQ", 0, 0), ("PQ", 0, 1), ("PQ", 0, 2),
+    ("QMW", 0, 5, 16), ("PQ", 0, 3), ("PQ", 0, 4), ("ADD", 0, 0), ("TS", 1, 1, 0), ("TS", 1, 2, 0),
+    ("TS", 1, 3, 0), ("ADD", 0, 1), ("ES", 1, 1, 0), ("PP", 0, 5), ("ES", 1, 2, 0), ("ADD", 0, 2),
+    ("TS", 1, 2, 1), ("ES", 1, 3, 0), ("PP", 0, 6), ("SIG", 0, 0, 1), ("TS", 1, 3, 1), ("QMS", 0, 5, 16),
+    ("ADD", 0, 3), ("ES", 1, 2, 1), ("PP", 0, 7), ("PQ", 0, 5), ("SIG", 0, 1, 1), ("PC", 0, 5),
+    ("ADD", 0, 4), ("PQ", 0, 6), ("SIG", 0, 3, 1), ("PC", 0, 6), ("PQ", 0, 7), ("ES", 1, 3, 1), ("PC", 0, 7),
+    ("ADD", 0, 5), ("PP", 0, 8), ("SIG", 0, 2, 1), ("PQ", 0, 8), ("PC", 0, 8), ("QS", 1, 1), ("XE", 0, 6),
+    ("PP", 0, 9), ("PQ", 0, 9), ("QS", 1, 3), ("PC", 0, 9), ("XE", 0, 8), ("XA", 0, 6), ("PP", 0, 10),
+    ("ADD", 0, 7), ("PQ", 0, 10), ("SIG", 0, 4, 1), ("PC", 0, 10), ("PA", 1), ("SIG", 0, 5, 1),
+    ("PP", 0, 11), ("QS", 1, 2), ("XA", 0, 8), ("PQ", 0, 11), ("SIG", 0, 7, 1), ("PC", 0, 11), ("QS", 1, 0),
+    ("ST", 0, 0), ("PP", 0, 12), ("XE", 0, 10), ("PQ", 0, 12), ("ADD", 0, 9), ("PC", 0, 12),
+    ("SIG", 0, 6, 1), ("PP", 0, 13), ("XA", 0, 10), ("PQ", 0, 13), ("ADD", 0, 11), ("PC", 0, 13),
+    ("XE", 0, 12), ("PP", 0, 14), ("PQ", 0, 14), ("SIG", 0, 8, 1), ("PC", 0, 14), ("XA", 0, 12), ("AA", 1),
+    ("PP", 0, 15), ("SIG", 0, 11, 1), ("PQ", 0, 15), ("PC", 0, 15), ("XE", 0, 14), ("QMW", 1, 0, 4),
+    ("PP", 1, 0), ("QMS", 1, 0, 4), ("PP", 1, 1), ("SIG", 0, 10, 1), ("ADD", 0, 13), ("ST", 0, 4),
+    ("XA", 0, 14), ("PQ", 1, 0), ("PC", 1, 0), ("SIG", 0, 9, 1), ("PQ", 1, 1), ("ADD", 0, 15), ("PC", 1, 1),
+    ("SIG", 0, 12, 1), ("PP", 1, 2), ("PQ", 1, 2), ("SIG", 0, 13, 1), ("PC", 1, 2), ("QMW", 1, 4, 16),
+    ("PP", 1, 3), ("SIG", 0, 15, 1), ("PQ", 1, 3), ("PC", 1, 3), ("XE", 1, 0), ("QMS", 1, 4, 16),
+    ("PP", 1, 4), ("ADD", 1, 1), ("PQ", 1, 4), ("SIG", 0, 14, 1), ("XA", 1, 0), ("PC", 1, 4), ("ST", 0, 8),
+    ("PP", 1, 5), ("XE", 1, 2), ("ADD", 1, 3), ("PQ", 1, 5), ("PC", 1, 5), ("SIG", 1, 1, 1), ("PP", 1, 6),
+    ("XA", 1, 2), ("PQ", 1, 6), ("XE", 1, 4), ("PC", 1, 6), ("ADD", 1, 5), ("PP", 1, 7), ("SIG", 1, 0, 1),
+    ("PQ", 1, 7), ("PC", 1, 7), ("XA", 1, 4), ("SIG", 1, 3, 1), ("PP", 1, 8), ("ST", 0, 12), ("PQ", 1, 8),
+    ("SIG", 1, 2, 1), ("PP", 1, 9), ("ADD", 1, 7), ("PC", 1, 8), ("SIG", 1, 5, 1), ("PQ", 1, 9),
+    ("PC", 1, 9), ("SIG", 1, 4, 1), ("PP", 1, 10), ("PQ", 1, 10), ("XE", 1, 6), ("PC", 1, 10), ("ADD", 1, 9),
+    ("SIG", 1, 7, 1), ("PP", 1, 12), ("XA", 1, 6), ("PP", 1, 11), ("XE", 1, 8), ("PQ", 1, 11), ("ST", 1, 0),
+    ("PC", 1, 11), ("XE", 1, 10), ("PQ", 1, 12), ("XA", 1, 8), ("PC", 1, 12), ("SIG", 1, 9, 1),
+    ("PP", 1, 13), ("ADD", 1, 11), ("PQ", 1, 13), ("SIG", 1, 6, 1), ("PC", 1, 13), ("PP", 1, 14),
+    ("XA", 1, 10), ("XE", 1, 12), ("PQ", 1, 14), ("PC", 1, 14), ("SIG", 1, 8, 1), ("ADD", 1, 13),
+    ("PP", 1, 15), ("PQ", 1, 15), ("SIG", 1, 11, 1), ("XA", 1, 12), ("PC", 1, 15), ("SIG", 1, 10, 1),
+    ("SIG", 1, 13, 1), ("ADD", 1, 15), ("ST", 1, 4), ("XE", 1, 14), ("SIG", 1, 12, 1), ("XA", 1, 14),
+    ("SIG", 1, 15, 1), ("ST", 1, 8), ("SIG", 1, 14, 1), ("ST", 1, 10), ("ST", 1, 12), ("ST", 1, 14),
+    ("ST", 1, 15),
 ]
 
 
@@ -76,12 +78,13 @@ def tile_differentiablelogicmachine_pa_kernel(tc, x1, x2, W2, b2, out):
     nc = tc.nc
     with ExitStack() as ctx:
         keep = ctx.enter_context(tc.tile_pool(name="keep", bufs=1))
-        grp_pool = ctx.enter_context(tc.tile_pool(name="grp", bufs=5))
+        grp_pool = ctx.enter_context(tc.tile_pool(name="grp", bufs=4))
         res_pools = {
             4: ctx.enter_context(tc.tile_pool(name="res4", bufs=5)),
             2: ctx.enter_context(tc.tile_pool(name="res2", bufs=3)),
             1: ctx.enter_context(tc.tile_pool(name="res1", bufs=2)),
         }
+        raw_pool = ctx.enter_context(tc.tile_pool(name="raw", bufs=3))
         tp_pool = ctx.enter_context(tc.psum_pool(name="tp", bufs=3))
         acc_pool = ctx.enter_context(tc.psum_pool(name="acc", bufs=5))
         ctx.enter_context(tc.manual_schedule())
@@ -135,6 +138,7 @@ def tile_differentiablelogicmachine_pa_kernel(tc, x1, x2, W2, b2, out):
         accs = {}
         passes = {}
         ress = {}
+        raws = {}
 
         def transposes(key, words):
             tps[key] = tp_pool.tile([P, 2, 2, P], F32, name="tp", tag="tp")
@@ -269,9 +273,19 @@ def tile_differentiablelogicmachine_pa_kernel(tc, x1, x2, W2, b2, out):
             elif op == "ADD":
                 h, j = step[1], step[2]
                 j0, size = group_of[(h, j)]
-                if j == j0:
+                if (h, j0) not in ress:
                     ress[(h, j0)] = res_pools[size].tile([P, size, OUT], F32, name="res", tag="res")
                 nc.vector.tensor_tensor(out=ress[(h, j0)][:, j - j0, :], in0=accs[(h, j)][:], in1=aprime[h][:], op=ADD)
+            elif op == "XE":
+                h, j = step[1], step[2]
+                raws[(h, j)] = raw_pool.tile([P, OUT], F32, name="raw", tag="raw")
+                nc.scalar.copy(out=raws[(h, j)][:], in_=accs[(h, j)][:])
+            elif op == "XA":
+                h, j = step[1], step[2]
+                j0, size = group_of[(h, j)]
+                if (h, j0) not in ress:
+                    ress[(h, j0)] = res_pools[size].tile([P, size, OUT], F32, name="res", tag="res")
+                nc.gpsimd.tensor_tensor(out=ress[(h, j0)][:, j - j0, :], in0=raws[(h, j)][:], in1=aprime[h][:], op=ADD)
             elif op == "SIG":
                 h, j, n = step[1], step[2], step[3]
                 j0, size = group_of[(h, j)]

@@ -13,142 +13,159 @@ ADD = mybir.AluOpType.add
 SIGMOID = mybir.ActivationFunctionType.Sigmoid
 
 P = 128
-NB = 16
-NO = 16
-CH = 512
+SCENES = 16
+OBJECTS = 16
+CHANNELS = 512
 OUT = 512
-HB = 8
+PACK = 4
+HALVES = 2
+HALF_SCENES = SCENES // HALVES
+SCALE_WORDS = HALF_SCENES // 4
 SLAB = 4
-NSLAB = NO // SLAB
+SLABS = OBJECTS // SLAB
+TILES = HALVES * OBJECTS
 
-FLOPS = 2 * NB * NO * NO * 4 * CH * OUT
+W_X1_I, W_X2_IJ, W_X1_J, W_X2_JI = 0, 1, 2, 3
 
-G_A, G_P, G_C, G_Q = 0, 1, 2, 3
+TRANSPOSE_BANKS = 3
+TILE_BANKS = 5
 
-GROUPS = [(0, 0, 4), (0, 4, 4), (0, 8, 4), (0, 12, 4), (1, 0, 4), (1, 4, 4), (1, 8, 2), (1, 10, 2), (1, 12, 2), (1, 14, 1), (1, 15, 1)]
+MOVE_PIECES = (((0, TILE_BANKS), (TILE_BANKS, OBJECTS)), ((0, SLAB), (SLAB, OBJECTS)))
+MOVE_LEAD = 3
 
-STEPS = [
-    ("LX1",), ("LW", 1), ("TX1",), ("LX", 0, 0), ("EX1",), ("RW", 1, "v"), ("LB2",), ("LW", 2),
-    ("TS", 0, 0, 0), ("LX", 0, 1), ("QX1",), ("TS", 0, 0, 1), ("QW", 1), ("ES", 0, 0, 0), ("CMW", 0, 0, 5),
-    ("LX", 0, 2), ("CMS", 0, 0, 5), ("ES", 0, 0, 1), ("CMW", 0, 5, 16), ("RW", 2, "s"), ("TS", 0, 1, 0),
-    ("LW", 3), ("QS", 0, 0), ("TS", 0, 1, 1), ("CMS", 0, 5, 16), ("CMS", 1, 0, 4), ("CMW", 1, 0, 4),
-    ("PP", 0, 0), ("LX", 0, 3), ("CMW", 1, 4, 16), ("TS", 0, 2, 0), ("PP", 0, 1), ("RW", 3, "v"),
-    ("ES", 0, 1, 0), ("LW", 0), ("PP", 0, 2), ("PP", 0, 3), ("ES", 0, 1, 1), ("TS", 0, 2, 1),
-    ("ES", 0, 2, 0), ("LX", 1, 0), ("QW", 2), ("TS", 0, 3, 0), ("QS", 0, 1), ("ES", 0, 2, 1),
-    ("TS", 0, 3, 1), ("LX", 1, 1), ("PC", 0, 0), ("RW", 0, "v"), ("ES", 0, 3, 0), ("PC", 0, 1),
-    ("ES", 0, 3, 1), ("MB2",), ("LX", 1, 2), ("PP", 0, 4), ("PC", 0, 2), ("QW", 0), ("EB2",),
-    ("TS", 1, 0, 0), ("QS", 0, 2), ("LX", 1, 3), ("PC", 0, 3), ("PC", 0, 4), ("QW", 3), ("ES", 1, 0, 0),
-    ("PA", 0), ("QS", 0, 3), ("TS", 1, 0, 1), ("TS", 1, 1, 1), ("CMS", 1, 4, 16), ("QMW", 0, 0, 5),
-    ("ES", 1, 0, 1), ("QMS", 0, 0, 5), ("AA", 0), ("ES", 1, 1, 1), ("PQ", 0, 0), ("PQ", 0, 1), ("PQ", 0, 2),
-    ("QMW", 0, 5, 16), ("PQ", 0, 3), ("PQ", 0, 4), ("ADD", 0, 0), ("TS", 1, 1, 0), ("TS", 1, 2, 0),
-    ("TS", 1, 3, 0), ("ADD", 0, 1), ("ES", 1, 1, 0), ("PP", 0, 5), ("ES", 1, 2, 0), ("ADD", 0, 2),
-    ("TS", 1, 2, 1), ("ES", 1, 3, 0), ("PP", 0, 6), ("SIG", 0, 0, 1), ("TS", 1, 3, 1), ("QMS", 0, 5, 16),
-    ("ADD", 0, 3), ("ES", 1, 2, 1), ("PP", 0, 7), ("PQ", 0, 5), ("SIG", 0, 1, 1), ("PC", 0, 5),
-    ("ADD", 0, 4), ("PQ", 0, 6), ("SIG", 0, 3, 1), ("PC", 0, 6), ("PQ", 0, 7), ("ES", 1, 3, 1), ("PC", 0, 7),
-    ("ADD", 0, 5), ("PP", 0, 8), ("SIG", 0, 2, 1), ("PQ", 0, 8), ("PC", 0, 8), ("QS", 1, 1), ("XE", 0, 6),
-    ("PP", 0, 9), ("PQ", 0, 9), ("QS", 1, 3), ("PC", 0, 9), ("XE", 0, 8), ("XA", 0, 6), ("PP", 0, 10),
-    ("ADD", 0, 7), ("PQ", 0, 10), ("SIG", 0, 4, 1), ("PC", 0, 10), ("PA", 1), ("SIG", 0, 5, 1),
-    ("PP", 0, 11), ("QS", 1, 2), ("XA", 0, 8), ("PQ", 0, 11), ("SIG", 0, 7, 1), ("PC", 0, 11), ("QS", 1, 0),
-    ("ST", 0, 0), ("PP", 0, 12), ("XE", 0, 10), ("PQ", 0, 12), ("ADD", 0, 9), ("PC", 0, 12),
-    ("SIG", 0, 6, 1), ("PP", 0, 13), ("XA", 0, 10), ("PQ", 0, 13), ("ADD", 0, 11), ("PC", 0, 13),
-    ("XE", 0, 12), ("PP", 0, 14), ("PQ", 0, 14), ("SIG", 0, 8, 1), ("PC", 0, 14), ("XA", 0, 12), ("AA", 1),
-    ("PP", 0, 15), ("SIG", 0, 11, 1), ("PQ", 0, 15), ("PC", 0, 15), ("XE", 0, 14), ("QMW", 1, 0, 4),
-    ("PP", 1, 0), ("QMS", 1, 0, 4), ("PP", 1, 1), ("SIG", 0, 10, 1), ("ADD", 0, 13), ("ST", 0, 4),
-    ("XA", 0, 14), ("PQ", 1, 0), ("PC", 1, 0), ("SIG", 0, 9, 1), ("PQ", 1, 1), ("ADD", 0, 15), ("PC", 1, 1),
-    ("SIG", 0, 12, 1), ("PP", 1, 2), ("PQ", 1, 2), ("SIG", 0, 13, 1), ("PC", 1, 2), ("QMW", 1, 4, 16),
-    ("PP", 1, 3), ("SIG", 0, 15, 1), ("PQ", 1, 3), ("PC", 1, 3), ("XE", 1, 0), ("QMS", 1, 4, 16),
-    ("PP", 1, 4), ("ADD", 1, 1), ("PQ", 1, 4), ("SIG", 0, 14, 1), ("XA", 1, 0), ("PC", 1, 4), ("ST", 0, 8),
-    ("PP", 1, 5), ("XE", 1, 2), ("ADD", 1, 3), ("PQ", 1, 5), ("PC", 1, 5), ("SIG", 1, 1, 1), ("PP", 1, 6),
-    ("XA", 1, 2), ("PQ", 1, 6), ("XE", 1, 4), ("PC", 1, 6), ("ADD", 1, 5), ("PP", 1, 7), ("SIG", 1, 0, 1),
-    ("PQ", 1, 7), ("PC", 1, 7), ("XA", 1, 4), ("SIG", 1, 3, 1), ("PP", 1, 8), ("ST", 0, 12), ("PQ", 1, 8),
-    ("SIG", 1, 2, 1), ("PP", 1, 9), ("ADD", 1, 7), ("PC", 1, 8), ("SIG", 1, 5, 1), ("PQ", 1, 9),
-    ("PC", 1, 9), ("SIG", 1, 4, 1), ("PP", 1, 10), ("PQ", 1, 10), ("XE", 1, 6), ("PC", 1, 10), ("ADD", 1, 9),
-    ("SIG", 1, 7, 1), ("PP", 1, 12), ("XA", 1, 6), ("PP", 1, 11), ("XE", 1, 8), ("PQ", 1, 11), ("ST", 1, 0),
-    ("PC", 1, 11), ("XE", 1, 10), ("PQ", 1, 12), ("XA", 1, 8), ("PC", 1, 12), ("SIG", 1, 9, 1),
-    ("PP", 1, 13), ("ADD", 1, 11), ("PQ", 1, 13), ("SIG", 1, 6, 1), ("PC", 1, 13), ("PP", 1, 14),
-    ("XA", 1, 10), ("XE", 1, 12), ("PQ", 1, 14), ("PC", 1, 14), ("SIG", 1, 8, 1), ("ADD", 1, 13),
-    ("PP", 1, 15), ("PQ", 1, 15), ("SIG", 1, 11, 1), ("XA", 1, 12), ("PC", 1, 15), ("SIG", 1, 10, 1),
-    ("SIG", 1, 13, 1), ("ADD", 1, 15), ("ST", 1, 4), ("XE", 1, 14), ("SIG", 1, 12, 1), ("XA", 1, 14),
-    ("SIG", 1, 15, 1), ("ST", 1, 8), ("SIG", 1, 14, 1), ("ST", 1, 10), ("ST", 1, 12), ("ST", 1, 14),
-    ("ST", 1, 15),
-]
+STORE_SIZES = (4, 4, 4, 4, 4, 4, 2, 2, 2, 1, 1)
+STORE_BUFS = ((4, 5), (2, 3), (1, 2))
+
+FLOPS = 2 * SCENES * OBJECTS * OBJECTS * 4 * CHANNELS * OUT
 
 
 def tile_differentiablelogicmachine_pa_kernel(tc, x1, x2, W2, b2, out):
     nc = tc.nc
     with ExitStack() as ctx:
         keep = ctx.enter_context(tc.tile_pool(name="keep", bufs=1))
-        grp_pool = ctx.enter_context(tc.tile_pool(name="grp", bufs=4))
-        res_pools = {
-            4: ctx.enter_context(tc.tile_pool(name="res4", bufs=5)),
-            2: ctx.enter_context(tc.tile_pool(name="res2", bufs=3)),
-            1: ctx.enter_context(tc.tile_pool(name="res1", bufs=2)),
-        }
-        raw_pool = ctx.enter_context(tc.tile_pool(name="raw", bufs=3))
-        tp_pool = ctx.enter_context(tc.psum_pool(name="tp", bufs=3))
-        acc_pool = ctx.enter_context(tc.psum_pool(name="acc", bufs=5))
-        ctx.enter_context(tc.manual_schedule())
+        grouped_pool = ctx.enter_context(tc.tile_pool(name="grouped", bufs=5))
+        result_pools = {}
+        for size, bufs in STORE_BUFS:
+            result_pools[size] = ctx.enter_context(tc.tile_pool(name="result%d" % size, bufs=bufs))
+        transpose_psum = ctx.enter_context(tc.psum_pool(name="transpose_psum", bufs=TRANSPOSE_BANKS))
+        tile_psum = ctx.enter_context(tc.psum_pool(name="tile_psum", bufs=TILE_BANKS))
 
-        ident = keep.tile([P, P], F32, name="ident")
+        identity = keep.tile([P, P], F32, name="identity")
         ones = keep.tile([P, P], BF16, name="ones")
-        b2row = keep.tile([P, OUT], BF16, name="b2row")
-        b2all = keep.tile([P, OUT], F32, name="b2all")
+        bias_row = keep.tile([P, OUT], BF16, name="bias_row")
+        bias_all = keep.tile([P, OUT], F32, name="bias_all")
         warm = keep.tile([P, 2], F32, name="warm")
-        x1_sb = keep.tile([P, 2, CH], BF16, name="x1_sb")
-        x1_grp = keep.tile([P, 2, P, 4], BF16, name="x1_grp", align_bytes=64)
-        x1_codes = keep.tile([P, 2, P], U32, name="x1_codes", align_bytes=64)
-        x1_scales = keep.tile([P, 2, P], U8, name="x1_scales", align_bytes=64)
-        w_raw = [keep.tile([P, 4, OUT], BF16, name="w_raw%d" % g) for g in range(4)]
-        w_grp = [keep.tile([P, OUT, 4], BF16, name="w_grp%d" % g, align_bytes=64) for g in range(4)]
+        x1_sb = keep.tile([P, HALVES, CHANNELS], BF16, name="x1_sb")
+        x1_grouped = keep.tile([P, HALVES, P, PACK], BF16, name="x1_grouped", align_bytes=64)
+        x1_codes = keep.tile([P, HALVES, P], U32, name="x1_codes", align_bytes=64)
+        x1_scales = keep.tile([P, HALVES, P], U8, name="x1_scales", align_bytes=64)
+        w_raw = [keep.tile([P, PACK, OUT], BF16, name="w_raw%d" % g) for g in range(4)]
+        w_grouped = [keep.tile([P, OUT, PACK], BF16, name="w_grouped%d" % g, align_bytes=64) for g in range(4)]
         w_codes = keep.tile([P, 4, OUT], U32, name="w_codes", align_bytes=64)
         w_scales = keep.tile([P, 4, OUT], U8, name="w_scales", align_bytes=64)
         x2_sb = [
-            [keep.tile([P, SLAB, CH], BF16, name="x2_sb%d_%d" % (h, s)) for s in range(NSLAB)]
-            for h in range(2)
+            [keep.tile([P, SLAB, CHANNELS], BF16, name="x2_sb%d_%d" % (h, s)) for s in range(SLABS)]
+            for h in range(HALVES)
         ]
-        p_codes = [keep.tile([P, NO, P], U32, name="p_codes%d" % h, align_bytes=64) for h in range(2)]
-        p_scales = [keep.tile([P, NO, P], U8, name="p_scales%d" % h, align_bytes=64) for h in range(2)]
-        q_codes = [keep.tile([P, NO, P], U32, name="q_codes%d" % h, align_bytes=64) for h in range(2)]
-        q_scales = [keep.tile([P, NO, P], U8, name="q_scales%d" % h, align_bytes=64) for h in range(2)]
-        c_codes = [keep.tile([P, NO, P], U32, name="c_codes%d" % h, align_bytes=64) for h in range(2)]
-        c_scales = [keep.tile([P, NO, P], U8, name="c_scales%d" % h, align_bytes=64) for h in range(2)]
-        aprime = [keep.tile([P, OUT], F32, name="aprime%d" % h) for h in range(2)]
 
-        x1_v = x1.rearrange("(h b) i k -> h i b k", h=2)
-        x2_v = x2.rearrange("(h b) i j k -> h i b (j k)", h=2)
-        w_v = W2.rearrange("(g u p e) o -> g p u (e o)", g=4, u=2, e=2)
-        out_v = out.rearrange("(h b) i j o -> h i b (j o)", h=2)
+        def operand(name):
+            codes = [keep.tile([P, OBJECTS, P], U32, name="%s_codes%d" % (name, h), align_bytes=64) for h in range(HALVES)]
+            scales = [keep.tile([P, OBJECTS, P], U8, name="%s_scales%d" % (name, h), align_bytes=64) for h in range(HALVES)]
+            return codes, scales
 
-        group_of = {}
-        for h, j0, size in GROUPS:
-            for j in range(j0, j0 + size):
-                group_of[(h, j)] = (j0, size)
+        ij_codes, ij_scales = operand("ij")
+        ji_codes, ji_scales = operand("ji")
+        xj_codes, xj_scales = operand("xj")
+        x1_term = [keep.tile([P, OUT], F32, name="x1_term%d" % h) for h in range(HALVES)]
 
-        nc.vector.memset(b2row[:], 0.0)
-        make_identity(nc, ident[:])
+        x1_view = x1.rearrange("(h b) i k -> h i b k", h=HALVES)
+        x2_view = x2.rearrange("(h b) i j k -> h i b (j k)", h=HALVES)
+        out_view = out.rearrange("(h b) i j o -> h i b (j o)", h=HALVES)
+        w_view = W2.rearrange("(g u p e) o -> g p u (e o)", g=4, u=2, e=2)
+
+        def load_weights(g):
+            nc.sync.dma_start(out=w_raw[g][:].rearrange("p (u e) o -> p u (e o)", u=2), in_=w_view[g])
+
+        def load_slab(h, s):
+            nc.sync.dma_start(
+                out=x2_sb[h][s][:].rearrange("p j k -> p (j k)"),
+                in_=x2_view[h][:, :, s * SLAB * CHANNELS : (s + 1) * SLAB * CHANNELS],
+            )
+
+        nc.vector.memset(bias_row[:], 0.0)
+        for h in range(HALVES):
+            nc.sync.dma_start(out=x1_sb[:, h, :], in_=x1_view[h])
+        load_weights(W_X2_IJ)
+        load_slab(0, 0)
+        nc.sync.dma_start(out=bias_row[0:1, :], in_=b2.unsqueeze(0))
+        load_weights(W_X1_J)
+        load_slab(0, 1)
+        load_slab(0, 2)
+        load_weights(W_X2_JI)
+        load_slab(0, 3)
+        load_weights(W_X1_I)
+        for s in range(SLABS):
+            load_slab(1, s)
+
+        make_identity(nc, identity[:])
         nc.vector.memset(ones[:], 1.0)
         nc.vector.memset(warm[:], 0.0)
         nc.scalar.activation(out=warm[:, 1:2], in_=warm[:, 0:1], func=SIGMOID)
         nc.vector.memset(x1_scales[:].bitcast(I32), 0)
-        for h in range(2):
-            nc.vector.memset(p_scales[h][:].bitcast(I32), 0)
+        for h in range(HALVES):
+            nc.vector.memset(ij_scales[h][:].bitcast(I32), 0)
 
-        tps = {}
-        grps = {}
-        accs = {}
-        passes = {}
-        ress = {}
-        raws = {}
-
-        def transposes(key, words):
-            tps[key] = tp_pool.tile([P, 2, 2, P], F32, name="tp", tag="tp")
-            for jj in range(2):
+        def transpose_two(rows_a, rows_b, grouped_words):
+            bank = transpose_psum.tile([P, 2, 2, P], F32, name="bank", tag="bank")
+            for block, rows in enumerate((rows_a, rows_b)):
                 for u in range(2):
-                    nc.tensor.transpose(tps[key][:, jj, u, :], words[jj][:, u * P : (u + 1) * P], ident[:])
+                    nc.tensor.transpose(bank[:, block, u, :], rows[:, u * P : (u + 1) * P], identity[:])
+            nc.scalar.copy(out=grouped_words, in_=bank[:].rearrange("p j u r -> p j r u"))
 
-        def mx(acc, codes, scales, g, start, stop):
+        def prepare_weights(g, on_vector):
+            dst = w_grouped[g][:].rearrange("p (c i) t -> p c t i", i=4)
+            src = w_raw[g][:].rearrange("p t (c i) -> p c t i", i=4)
+            if on_vector:
+                nc.vector.tensor_copy(out=dst, in_=src)
+            else:
+                nc.scalar.copy(out=dst, in_=src)
+            nc.vector.quantize_mx(
+                out=w_codes[:, g, :].bitcast(FP8X4),
+                scales=w_scales[:, g, :],
+                in_=w_grouped[g][:].rearrange("p o t -> p (o t)"),
+            )
+
+        def prepare_slab(h, s):
+            words = x2_sb[h][s][:].bitcast(F32)
+            grouped = grouped_pool.tile([P, SLAB, P, PACK], BF16, name="grouped", tag="grouped", align_bytes=64)
+            grouped_words = grouped[:].bitcast(F32)
+            for first in range(0, SLAB, 2):
+                transpose_two(words[:, first, :], words[:, first + 1, :], grouped_words[:, first : first + 2, :, :])
+            blocks = slice(s * SLAB, (s + 1) * SLAB)
+            nc.vector.quantize_mx(
+                out=ij_codes[h][:, blocks, :].rearrange("p j r -> p (j r)").bitcast(FP8X4),
+                scales=ij_scales[h][:, blocks, :].rearrange("p j r -> p (j r)"),
+                in_=grouped[:].rearrange("p j r t -> p (j r t)"),
+            )
+
+        def repeat_x1(h, lo, hi):
+            for dst, src, run in ((xj_codes, x1_codes, HALF_SCENES), (xj_scales, x1_scales, SCALE_WORDS)):
+                nc.vector.tensor_copy(
+                    out=dst[h][:, lo:hi, :].bitcast(I32).rearrange("p j (i w) -> p j i w", w=run),
+                    in_=src[:, h, lo * HALF_SCENES : hi * HALF_SCENES].bitcast(I32)
+                    .rearrange("p (j w) -> p j w", w=run).unsqueeze(2).to_broadcast([P, hi - lo, OBJECTS, run]),
+                )
+
+        def swap_x2(h, lo, hi):
+            for dst, src, run in ((ji_codes, ij_codes, HALF_SCENES), (ji_scales, ij_scales, SCALE_WORDS)):
+                nc.vector.tensor_copy(
+                    out=dst[h][:, lo:hi, :].bitcast(I32).rearrange("p j (i w) -> p j i w", w=run),
+                    in_=src[h][:].bitcast(I32).rearrange("p i (j w) -> p j i w", w=run)[:, lo:hi, :, :],
+                )
+
+        def mx_pass(bank, codes, scales, g, start, stop):
             nc.tensor.matmul_mx(
-                out=acc,
+                out=bank,
                 lhsT=codes.bitcast(FP8X4),
                 lhsT_scale=scales,
                 rhs=w_codes[:, g, :].bitcast(FP8X4),
@@ -157,146 +174,94 @@ def tile_differentiablelogicmachine_pa_kernel(tc, x1, x2, W2, b2, out):
                 stop=stop,
             )
 
-        def tile_pass(h, j, codes, scales, g):
-            done = passes.get((h, j), 0)
-            if done == 0:
-                accs[(h, j)] = acc_pool.tile([P, OUT], F32, name="acc", tag="acc")
-            mx(accs[(h, j)][:], codes[h][:, j, :], scales[h][:, j, :], g, done == 0, done == 2)
-            passes[(h, j)] = done + 1
+        def prepare_x1_term(h):
+            bank = transpose_psum.tile([P, OUT], F32, name="x1_bank", tag="bank")
+            mx_pass(bank[:], x1_codes[:, h, :], x1_scales[:, h, :], W_X1_I, True, True)
+            nc.vector.tensor_tensor(out=x1_term[h][:], in0=bank[:], in1=bias_all[:], op=ADD)
 
-        for step in STEPS:
-            op = step[0]
-            if op == "LX1":
-                for h in range(2):
-                    nc.sync.dma_start(out=x1_sb[:, h, :], in_=x1_v[h])
-            elif op == "LB2":
-                nc.sync.dma_start(out=b2row[0:1, :], in_=b2.unsqueeze(0))
-            elif op == "LW":
-                g = step[1]
-                nc.sync.dma_start(out=w_raw[g][:].rearrange("p (u e) o -> p u (e o)", u=2), in_=w_v[g])
-            elif op == "LX":
-                h, s = step[1], step[2]
+        banks = {}
+
+        def pass_ij(n):
+            h, j = divmod(n, OBJECTS)
+            banks[n] = tile_psum.tile([P, OUT], F32, name="tile_bank", tag="tile_bank")
+            mx_pass(banks[n][:], ij_codes[h][:, j, :], ij_scales[h][:, j, :], W_X2_IJ, True, False)
+
+        def pass_xj(n):
+            h, j = divmod(n, OBJECTS)
+            mx_pass(banks[n][:], xj_codes[h][:, j, :], xj_scales[h][:, j, :], W_X1_J, False, False)
+
+        def pass_ji(n):
+            h, j = divmod(n, OBJECTS)
+            mx_pass(banks[n][:], ji_codes[h][:, j, :], ji_scales[h][:, j, :], W_X2_JI, False, True)
+
+        store_of = {}
+        first = 0
+        for size in STORE_SIZES:
+            for n in range(first, first + size):
+                store_of[n] = (first, size)
+            first += size
+        results = {}
+
+        def finish(n):
+            first_n, size = store_of[n]
+            if n == first_n:
+                results[first_n] = result_pools[size].tile([P, size, OUT], F32, name="result", tag="result")
+            h, j = divmod(n, OBJECTS)
+            part = results[first_n][:, n - first_n, :]
+            nc.vector.tensor_tensor(out=part, in0=banks[n][:], in1=x1_term[h][:], op=ADD)
+            if n == first_n + size - 1:
+                whole = results[first_n][:].rearrange("p j o -> p (j o)")
+                nc.scalar.activation(out=whole, in_=whole, func=SIGMOID)
                 nc.sync.dma_start(
-                    out=x2_sb[h][s][:].rearrange("p j k -> p (j k)"),
-                    in_=x2_v[h][:, :, s * SLAB * CH : (s + 1) * SLAB * CH],
+                    out=out_view[h][:, :, (j + 1 - size) * OUT : (j + 1) * OUT],
+                    in_=results[first_n][:].rearrange("p j o -> p (j o)"),
                 )
-            elif op == "MB2":
-                tps["b2"] = tp_pool.tile([P, OUT], F32, name="b2_ps", tag="tp")
-                nc.tensor.matmul(tps["b2"][:], lhsT=ones[:], rhs=b2row[:], start=True, stop=True)
-            elif op == "EB2":
-                nc.scalar.copy(out=b2all[:], in_=tps["b2"][:])
-            elif op == "TX1":
-                x1_words = x1_sb[:].bitcast(F32)
-                transposes("x1", [x1_words[:, h, :] for h in range(2)])
-            elif op == "EX1":
-                nc.scalar.copy(out=x1_grp[:].bitcast(F32), in_=tps["x1"][:].rearrange("p j u r -> p j r u"))
-            elif op == "QX1":
-                nc.vector.quantize_mx(
-                    out=x1_codes[:].rearrange("p h r -> p (h r)").bitcast(FP8X4),
-                    scales=x1_scales[:].rearrange("p h r -> p (h r)"),
-                    in_=x1_grp[:].rearrange("p h r t -> p (h r t)"),
-                )
-            elif op == "RW":
-                g = step[1]
-                dst = w_grp[g][:].rearrange("p (c i) t -> p c t i", i=4)
-                src = w_raw[g][:].rearrange("p t (c i) -> p c t i", i=4)
-                if step[2] == "v":
-                    nc.vector.tensor_copy(out=dst, in_=src)
-                else:
-                    nc.scalar.copy(out=dst, in_=src)
-            elif op == "QW":
-                g = step[1]
-                nc.vector.quantize_mx(
-                    out=w_codes[:, g, :].bitcast(FP8X4),
-                    scales=w_scales[:, g, :],
-                    in_=w_grp[g][:].rearrange("p o t -> p (o t)"),
-                )
-            elif op == "TS":
-                h, s, half = step[1], step[2], step[3]
-                words = x2_sb[h][s][:].bitcast(F32)
-                transposes((h, s, half), [words[:, 2 * half + jj, :] for jj in range(2)])
-            elif op == "ES":
-                h, s, half = step[1], step[2], step[3]
-                if (h, s) not in grps:
-                    grps[(h, s)] = grp_pool.tile([P, SLAB, P, 4], BF16, name="x2_grp", tag="x2_grp", align_bytes=64)
-                nc.scalar.copy(
-                    out=grps[(h, s)][:].bitcast(F32)[:, 2 * half : 2 * half + 2, :, :],
-                    in_=tps[(h, s, half)][:].rearrange("p j u r -> p j r u"),
-                )
-            elif op == "QS":
-                h, s = step[1], step[2]
-                lo, hi = s * SLAB, (s + 1) * SLAB
-                nc.vector.quantize_mx(
-                    out=p_codes[h][:, lo:hi, :].rearrange("p j r -> p (j r)").bitcast(FP8X4),
-                    scales=p_scales[h][:, lo:hi, :].rearrange("p j r -> p (j r)"),
-                    in_=grps[(h, s)][:].rearrange("p j r t -> p (j r t)"),
-                )
-            elif op == "QMW":
-                h, lo, hi = step[1], step[2], step[3]
-                nc.vector.tensor_copy(
-                    out=q_codes[h][:, lo:hi, :].bitcast(I32).rearrange("p j (i b) -> p j i b", b=HB),
-                    in_=p_codes[h][:].bitcast(I32).rearrange("p i (j b) -> p j i b", b=HB)[:, lo:hi, :, :],
-                )
-            elif op == "QMS":
-                h, lo, hi = step[1], step[2], step[3]
-                nc.vector.tensor_copy(
-                    out=q_scales[h][:, lo:hi, :].bitcast(I32).rearrange("p j (i w) -> p j i w", w=2),
-                    in_=p_scales[h][:].bitcast(I32).rearrange("p i (j w) -> p j i w", w=2)[:, lo:hi, :, :],
-                )
-            elif op == "CMW":
-                h, lo, hi = step[1], step[2], step[3]
-                nc.vector.tensor_copy(
-                    out=c_codes[h][:, lo:hi, :].bitcast(I32).rearrange("p j (i b) -> p j i b", b=HB),
-                    in_=x1_codes[:, h, lo * HB : hi * HB].bitcast(I32).rearrange("p (j b) -> p j b", b=HB)
-                    .unsqueeze(2).to_broadcast([P, hi - lo, NO, HB]),
-                )
-            elif op == "CMS":
-                h, lo, hi = step[1], step[2], step[3]
-                nc.vector.tensor_copy(
-                    out=c_scales[h][:, lo:hi, :].bitcast(I32).rearrange("p j (i w) -> p j i w", w=2),
-                    in_=x1_scales[:, h, lo * HB : hi * HB].bitcast(I32).rearrange("p (j w) -> p j w", w=2)
-                    .unsqueeze(2).to_broadcast([P, hi - lo, NO, 2]),
-                )
-            elif op == "PP":
-                tile_pass(step[1], step[2], p_codes, p_scales, G_P)
-            elif op == "PC":
-                tile_pass(step[1], step[2], c_codes, c_scales, G_C)
-            elif op == "PQ":
-                tile_pass(step[1], step[2], q_codes, q_scales, G_Q)
-            elif op == "PA":
-                h = step[1]
-                tps[("a", h)] = tp_pool.tile([P, OUT], F32, name="a_ps", tag="tp")
-                mx(tps[("a", h)][:], x1_codes[:, h, :], x1_scales[:, h, :], G_A, True, True)
-            elif op == "AA":
-                h = step[1]
-                nc.vector.tensor_tensor(out=aprime[h][:], in0=tps[("a", h)][:], in1=b2all[:], op=ADD)
-            elif op == "ADD":
-                h, j = step[1], step[2]
-                j0, size = group_of[(h, j)]
-                if (h, j0) not in ress:
-                    ress[(h, j0)] = res_pools[size].tile([P, size, OUT], F32, name="res", tag="res")
-                nc.vector.tensor_tensor(out=ress[(h, j0)][:, j - j0, :], in0=accs[(h, j)][:], in1=aprime[h][:], op=ADD)
-            elif op == "XE":
-                h, j = step[1], step[2]
-                raws[(h, j)] = raw_pool.tile([P, OUT], F32, name="raw", tag="raw")
-                nc.scalar.copy(out=raws[(h, j)][:], in_=accs[(h, j)][:])
-            elif op == "XA":
-                h, j = step[1], step[2]
-                j0, size = group_of[(h, j)]
-                if (h, j0) not in ress:
-                    ress[(h, j0)] = res_pools[size].tile([P, size, OUT], F32, name="res", tag="res")
-                nc.gpsimd.tensor_tensor(out=ress[(h, j0)][:, j - j0, :], in0=raws[(h, j)][:], in1=aprime[h][:], op=ADD)
-            elif op == "SIG":
-                h, j, n = step[1], step[2], step[3]
-                j0, size = group_of[(h, j)]
-                part = ress[(h, j0)][:, j - j0 : j - j0 + n, :]
-                nc.scalar.activation(out=part, in_=part, func=SIGMOID)
-            elif op == "ST":
-                h, j0 = step[1], step[2]
-                size = group_of[(h, j0)][1]
-                nc.sync.dma_start(
-                    out=out_v[h][:, :, j0 * OUT : (j0 + size) * OUT],
-                    in_=ress[(h, j0)][:].rearrange("p j o -> p (j o)"),
-                )
-            else:
-                raise ValueError(op)
+
+        x1_words = x1_sb[:].bitcast(F32)
+        transpose_two(x1_words[:, 0, :], x1_words[:, 1, :], x1_grouped[:].bitcast(F32))
+        prepare_weights(W_X2_IJ, True)
+        nc.vector.quantize_mx(
+            out=x1_codes[:].rearrange("p h r -> p (h r)").bitcast(FP8X4),
+            scales=x1_scales[:].rearrange("p h r -> p (h r)"),
+            in_=x1_grouped[:].rearrange("p h r t -> p (h r t)"),
+        )
+        prepare_slab(0, 0)
+        repeat_x1(0, *MOVE_PIECES[0][0])
+        prepare_weights(W_X1_J, False)
+        prepare_slab(0, 1)
+        for n in range(TILE_BANKS):
+            pass_ij(n)
+        for n in range(TILE_BANKS):
+            pass_xj(n)
+        prepare_slab(0, 2)
+        prepare_weights(W_X2_JI, True)
+        prepare_slab(0, 3)
+        swap_x2(0, *MOVE_PIECES[0][0])
+        for n in range(TILE_BANKS):
+            pass_ji(n)
+        bias_bank = transpose_psum.tile([P, OUT], F32, name="bias_bank", tag="bank")
+        nc.tensor.matmul(bias_bank[:], lhsT=ones[:], rhs=bias_row[:], start=True, stop=True)
+        nc.scalar.copy(out=bias_all[:], in_=bias_bank[:])
+        prepare_weights(W_X1_I, True)
+        prepare_x1_term(0)
+
+        later_pieces = {}
+        for h in range(HALVES):
+            for lo, hi in MOVE_PIECES[h]:
+                if (h, lo) != (0, 0):
+                    later_pieces[max(0, h * OBJECTS + lo - TILE_BANKS - MOVE_LEAD)] = (h, lo, hi)
+        for n in range(TILES):
+            if n < SLABS:
+                prepare_slab(1, n)
+            if n in later_pieces:
+                h, lo, hi = later_pieces[n]
+                if (h, lo) == (1, 0):
+                    prepare_x1_term(1)
+                repeat_x1(h, lo, hi)
+                swap_x2(h, lo, hi)
+            finish(n)
+            ahead = n + TILE_BANKS
+            if ahead < TILES:
+                pass_ij(ahead)
+                pass_xj(ahead)
+                pass_ji(ahead)

@@ -30,8 +30,9 @@ W_X1_I, W_X2_IJ, W_X1_J, W_X2_JI = 0, 1, 2, 3
 TRANSPOSE_BANKS = 3
 TILE_BANKS = 5
 
-MOVE_PIECES = (((0, TILE_BANKS), (TILE_BANKS, OBJECTS)), ((0, SLAB), (SLAB, OBJECTS)))
-MOVE_LEAD = 3
+SWAP_PIECES = (((0, TILE_BANKS), (TILE_BANKS, OBJECTS)), ((0, SLAB), (SLAB, OBJECTS)))
+SWAP_AFTER_TILE = (7, 13)
+SECOND_X1_TERM_AFTER_TILE = 5
 
 STORE_SIZES = (4, 4, 4, 4, 4, 4, 2, 2, 2, 1, 1)
 STORE_BUFS = ((4, 5), (2, 3), (1, 2))
@@ -49,6 +50,7 @@ def tile_differentiablelogicmachine_pa_kernel(tc, x1, x2, W2, b2, out):
             result_pools[size] = ctx.enter_context(tc.tile_pool(name="result%d" % size, bufs=bufs))
         transpose_psum = ctx.enter_context(tc.psum_pool(name="transpose_psum", bufs=TRANSPOSE_BANKS))
         tile_psum = ctx.enter_context(tc.psum_pool(name="tile_psum", bufs=TILE_BANKS))
+        ctx.enter_context(tc.manual_schedule())
 
         identity = keep.tile([P, P], F32, name="identity")
         ones = keep.tile([P, P], BF16, name="ones")
@@ -122,30 +124,36 @@ def tile_differentiablelogicmachine_pa_kernel(tc, x1, x2, W2, b2, out):
                     nc.tensor.transpose(bank[:, block, u, :], rows[:, u * P : (u + 1) * P], identity[:])
             nc.scalar.copy(out=grouped_words, in_=bank[:].rearrange("p j u r -> p j r u"))
 
-        def prepare_weights(g, on_vector):
+        def regroup_weights(g, on_vector):
             dst = w_grouped[g][:].rearrange("p (c i) t -> p c t i", i=4)
             src = w_raw[g][:].rearrange("p t (c i) -> p c t i", i=4)
             if on_vector:
                 nc.vector.tensor_copy(out=dst, in_=src)
             else:
                 nc.scalar.copy(out=dst, in_=src)
+
+        def quantise_weights(g):
             nc.vector.quantize_mx(
                 out=w_codes[:, g, :].bitcast(FP8X4),
                 scales=w_scales[:, g, :],
                 in_=w_grouped[g][:].rearrange("p o t -> p (o t)"),
             )
 
-        def prepare_slab(h, s):
+        grouped_of = {}
+
+        def transpose_slab(h, s):
             words = x2_sb[h][s][:].bitcast(F32)
-            grouped = grouped_pool.tile([P, SLAB, P, PACK], BF16, name="grouped", tag="grouped", align_bytes=64)
-            grouped_words = grouped[:].bitcast(F32)
-            for first in range(0, SLAB, 2):
-                transpose_two(words[:, first, :], words[:, first + 1, :], grouped_words[:, first : first + 2, :, :])
+            grouped_of[(h, s)] = grouped_pool.tile([P, SLAB, P, PACK], BF16, name="grouped", tag="grouped", align_bytes=64)
+            grouped_words = grouped_of[(h, s)][:].bitcast(F32)
+            for block in range(0, SLAB, 2):
+                transpose_two(words[:, block, :], words[:, block + 1, :], grouped_words[:, block : block + 2, :, :])
+
+        def quantise_slab(h, s):
             blocks = slice(s * SLAB, (s + 1) * SLAB)
             nc.vector.quantize_mx(
                 out=ij_codes[h][:, blocks, :].rearrange("p j r -> p (j r)").bitcast(FP8X4),
                 scales=ij_scales[h][:, blocks, :].rearrange("p j r -> p (j r)"),
-                in_=grouped[:].rearrange("p j r t -> p (j r t)"),
+                in_=grouped_of[(h, s)][:].rearrange("p j r t -> p (j r t)"),
             )
 
         def repeat_x1(h, lo, hi):
@@ -174,10 +182,14 @@ def tile_differentiablelogicmachine_pa_kernel(tc, x1, x2, W2, b2, out):
                 stop=stop,
             )
 
-        def prepare_x1_term(h):
-            bank = transpose_psum.tile([P, OUT], F32, name="x1_bank", tag="bank")
-            mx_pass(bank[:], x1_codes[:, h, :], x1_scales[:, h, :], W_X1_I, True, True)
-            nc.vector.tensor_tensor(out=x1_term[h][:], in0=bank[:], in1=bias_all[:], op=ADD)
+        x1_banks = {}
+
+        def x1_term_pass(h):
+            x1_banks[h] = transpose_psum.tile([P, OUT], F32, name="x1_bank", tag="bank")
+            mx_pass(x1_banks[h][:], x1_codes[:, h, :], x1_scales[:, h, :], W_X1_I, True, True)
+
+        def x1_term_add(h):
+            nc.vector.tensor_tensor(out=x1_term[h][:], in0=x1_banks[h][:], in1=bias_all[:], op=ADD)
 
         banks = {}
 
@@ -202,16 +214,20 @@ def tile_differentiablelogicmachine_pa_kernel(tc, x1, x2, W2, b2, out):
             first += size
         results = {}
 
-        def finish(n):
+        def add_x1_term(n):
             first_n, size = store_of[n]
             if n == first_n:
                 results[first_n] = result_pools[size].tile([P, size, OUT], F32, name="result", tag="result")
-            h, j = divmod(n, OBJECTS)
+            nc.vector.tensor_tensor(
+                out=results[first_n][:, n - first_n, :], in0=banks[n][:], in1=x1_term[n // OBJECTS][:], op=ADD
+            )
+
+        def sigmoid_and_store(n):
+            first_n, size = store_of[n]
             part = results[first_n][:, n - first_n, :]
-            nc.vector.tensor_tensor(out=part, in0=banks[n][:], in1=x1_term[h][:], op=ADD)
+            nc.scalar.activation(out=part, in_=part, func=SIGMOID)
             if n == first_n + size - 1:
-                whole = results[first_n][:].rearrange("p j o -> p (j o)")
-                nc.scalar.activation(out=whole, in_=whole, func=SIGMOID)
+                h, j = divmod(n, OBJECTS)
                 nc.sync.dma_start(
                     out=out_view[h][:, :, (j + 1 - size) * OUT : (j + 1) * OUT],
                     in_=results[first_n][:].rearrange("p j o -> p (j o)"),
@@ -219,47 +235,56 @@ def tile_differentiablelogicmachine_pa_kernel(tc, x1, x2, W2, b2, out):
 
         x1_words = x1_sb[:].bitcast(F32)
         transpose_two(x1_words[:, 0, :], x1_words[:, 1, :], x1_grouped[:].bitcast(F32))
-        prepare_weights(W_X2_IJ, True)
+        regroup_weights(W_X2_IJ, True)
         nc.vector.quantize_mx(
             out=x1_codes[:].rearrange("p h r -> p (h r)").bitcast(FP8X4),
             scales=x1_scales[:].rearrange("p h r -> p (h r)"),
             in_=x1_grouped[:].rearrange("p h r t -> p (h r t)"),
         )
-        prepare_slab(0, 0)
-        repeat_x1(0, *MOVE_PIECES[0][0])
-        prepare_weights(W_X1_J, False)
-        prepare_slab(0, 1)
+        quantise_weights(W_X2_IJ)
+        regroup_weights(W_X1_J, False)
+        for h in range(HALVES):
+            repeat_x1(h, 0, OBJECTS)
+        transpose_slab(0, 0)
+        quantise_weights(W_X1_J)
+        regroup_weights(W_X2_JI, True)
+        quantise_slab(0, 0)
+        transpose_slab(0, 1)
+        quantise_weights(W_X2_JI)
+        regroup_weights(W_X1_I, True)
+        quantise_slab(0, 1)
+        transpose_slab(0, 2)
+        quantise_weights(W_X1_I)
+        quantise_slab(0, 2)
+        transpose_slab(0, 3)
+        quantise_slab(0, 3)
+        bias_bank = transpose_psum.tile([P, OUT], F32, name="bias_bank", tag="bank")
+        nc.tensor.matmul(bias_bank[:], lhsT=ones[:], rhs=bias_row[:], start=True, stop=True)
+        nc.scalar.copy(out=bias_all[:], in_=bias_bank[:])
         for n in range(TILE_BANKS):
             pass_ij(n)
         for n in range(TILE_BANKS):
             pass_xj(n)
-        prepare_slab(0, 2)
-        prepare_weights(W_X2_JI, True)
-        prepare_slab(0, 3)
-        swap_x2(0, *MOVE_PIECES[0][0])
+        x1_term_pass(0)
+        swap_x2(0, *SWAP_PIECES[0][0])
+        x1_term_add(0)
+        transpose_slab(1, 0)
         for n in range(TILE_BANKS):
             pass_ji(n)
-        bias_bank = transpose_psum.tile([P, OUT], F32, name="bias_bank", tag="bank")
-        nc.tensor.matmul(bias_bank[:], lhsT=ones[:], rhs=bias_row[:], start=True, stop=True)
-        nc.scalar.copy(out=bias_all[:], in_=bias_bank[:])
-        prepare_weights(W_X1_I, True)
-        prepare_x1_term(0)
+        swap_x2(0, *SWAP_PIECES[0][1])
 
-        later_pieces = {}
-        for h in range(HALVES):
-            for lo, hi in MOVE_PIECES[h]:
-                if (h, lo) != (0, 0):
-                    later_pieces[max(0, h * OBJECTS + lo - TILE_BANKS - MOVE_LEAD)] = (h, lo, hi)
         for n in range(TILES):
-            if n < SLABS:
-                prepare_slab(1, n)
-            if n in later_pieces:
-                h, lo, hi = later_pieces[n]
-                if (h, lo) == (1, 0):
-                    prepare_x1_term(1)
-                repeat_x1(h, lo, hi)
-                swap_x2(h, lo, hi)
-            finish(n)
+            if n + 1 < SLABS:
+                transpose_slab(1, n + 1)
+            add_x1_term(n)
+            if 1 <= n <= SLABS:
+                quantise_slab(1, n - 1)
+            if n == SECOND_X1_TERM_AFTER_TILE:
+                x1_term_pass(1)
+                x1_term_add(1)
+            if n in SWAP_AFTER_TILE:
+                swap_x2(1, *SWAP_PIECES[1][SWAP_AFTER_TILE.index(n)])
+            sigmoid_and_store(n)
             ahead = n + TILE_BANKS
             if ahead < TILES:
                 pass_ij(ahead)

@@ -219,7 +219,7 @@ def tile_differentiablelogicmachine_pa_kernel(tc, x1, x2, W2, b2, out):
             if n == first_n:
                 results[first_n] = result_pools[size].tile([P, size, OUT], F32, name="result", tag="result")
             nc.vector.tensor_tensor(
-                out=results[first_n][:, n - first_n, :], in0=banks[n][:], in1=x1_term[n // OBJECTS][:], op=ADD
+                out=results[first_n][:, n - first_n, :], in0=x1_term[n // OBJECTS][:], in1=banks[n][:], op=ADD
             )
 
         def sigmoid_and_store(n):

from contextlib import ExitStack

import concourse.mybir as mybir
from concourse.masks import make_identity

F32 = mybir.dt.float32
BF16 = mybir.dt.bfloat16
U32 = mybir.dt.uint32
I32 = mybir.dt.int32
U8 = mybir.dt.uint8
FP8X4 = mybir.dt.float8_e4m3fn_x4
ADD = mybir.AluOpType.add
SIGMOID = mybir.ActivationFunctionType.Sigmoid

P = 128
SCENES = 16
OBJECTS = 16
CHANNELS = 512
OUT = 512
PACK = 4
HALVES = 2
HALF_SCENES = SCENES // HALVES
SCALE_WORDS = HALF_SCENES // 4
SLAB = 4
SLABS = OBJECTS // SLAB
TILES = HALVES * OBJECTS

W_X1_I, W_X2_IJ, W_X1_J, W_X2_JI = 0, 1, 2, 3

TRANSPOSE_BANKS = 3
TILE_BANKS = 5

SWAP_PIECES = (((0, TILE_BANKS), (TILE_BANKS, OBJECTS)), ((0, SLAB), (SLAB, OBJECTS)))
SWAP_AFTER_TILE = (7, 13)
SECOND_X1_TERM_AFTER_TILE = 5

STORE_SIZES = (4, 4, 4, 4, 4, 4, 2, 2, 2, 1, 1)
STORE_BUFS = ((4, 5), (2, 3), (1, 2))

FLOPS = 2 * SCENES * OBJECTS * OBJECTS * 4 * CHANNELS * OUT


def tile_differentiablelogicmachine_pa_kernel(tc, x1, x2, W2, b2, out):
    nc = tc.nc
    with ExitStack() as ctx:
        keep = ctx.enter_context(tc.tile_pool(name="keep", bufs=1))
        grouped_pool = ctx.enter_context(tc.tile_pool(name="grouped", bufs=5))
        result_pools = {}
        for size, bufs in STORE_BUFS:
            result_pools[size] = ctx.enter_context(tc.tile_pool(name="result%d" % size, bufs=bufs))
        transpose_psum = ctx.enter_context(tc.psum_pool(name="transpose_psum", bufs=TRANSPOSE_BANKS))
        tile_psum = ctx.enter_context(tc.psum_pool(name="tile_psum", bufs=TILE_BANKS))
        ctx.enter_context(tc.manual_schedule())

        identity = keep.tile([P, P], F32, name="identity")
        ones = keep.tile([P, P], BF16, name="ones")
        bias_row = keep.tile([P, OUT], BF16, name="bias_row")
        bias_all = keep.tile([P, OUT], F32, name="bias_all")
        warm = keep.tile([P, 2], F32, name="warm")
        x1_sb = keep.tile([P, HALVES, CHANNELS], BF16, name="x1_sb")
        x1_grouped = keep.tile([P, HALVES, P, PACK], BF16, name="x1_grouped", align_bytes=64)
        x1_codes = keep.tile([P, HALVES, P], U32, name="x1_codes", align_bytes=64)
        x1_scales = keep.tile([P, HALVES, P], U8, name="x1_scales", align_bytes=64)
        w_raw = [keep.tile([P, PACK, OUT], BF16, name="w_raw%d" % g) for g in range(4)]
        w_grouped = [keep.tile([P, OUT, PACK], BF16, name="w_grouped%d" % g, align_bytes=64) for g in range(4)]
        w_codes = keep.tile([P, 4, OUT], U32, name="w_codes", align_bytes=64)
        w_scales = keep.tile([P, 4, OUT], U8, name="w_scales", align_bytes=64)
        x2_sb = [
            [keep.tile([P, SLAB, CHANNELS], BF16, name="x2_sb%d_%d" % (h, s)) for s in range(SLABS)]
            for h in range(HALVES)
        ]

        def operand(name):
            codes = [keep.tile([P, OBJECTS, P], U32, name="%s_codes%d" % (name, h), align_bytes=64) for h in range(HALVES)]
            scales = [keep.tile([P, OBJECTS, P], U8, name="%s_scales%d" % (name, h), align_bytes=64) for h in range(HALVES)]
            return codes, scales

        ij_codes, ij_scales = operand("ij")
        ji_codes, ji_scales = operand("ji")
        xj_codes, xj_scales = operand("xj")
        x1_term = [keep.tile([P, OUT], F32, name="x1_term%d" % h) for h in range(HALVES)]

        x1_view = x1.rearrange("(h b) i k -> h i b k", h=HALVES)
        x2_view = x2.rearrange("(h b) i j k -> h i b (j k)", h=HALVES)
        out_view = out.rearrange("(h b) i j o -> h i b (j o)", h=HALVES)
        w_view = W2.rearrange("(g u p e) o -> g p u (e o)", g=4, u=2, e=2)

        def load_weights(g):
            nc.sync.dma_start(out=w_raw[g][:].rearrange("p (u e) o -> p u (e o)", u=2), in_=w_view[g])

        def load_slab(h, s):
            nc.sync.dma_start(
                out=x2_sb[h][s][:].rearrange("p j k -> p (j k)"),
                in_=x2_view[h][:, :, s * SLAB * CHANNELS : (s + 1) * SLAB * CHANNELS],
            )

        nc.vector.memset(bias_row[:], 0.0)
        for h in range(HALVES):
            nc.sync.dma_start(out=x1_sb[:, h, :], in_=x1_view[h])
        load_weights(W_X2_IJ)
        load_slab(0, 0)
        nc.sync.dma_start(out=bias_row[0:1, :], in_=b2.unsqueeze(0))
        load_weights(W_X1_J)
        load_slab(0, 1)
        load_slab(0, 2)
        load_weights(W_X2_JI)
        load_slab(0, 3)
        load_weights(W_X1_I)
        for s in range(SLABS):
            load_slab(1, s)

        make_identity(nc, identity[:])
        nc.vector.memset(ones[:], 1.0)
        nc.vector.memset(warm[:], 0.0)
        nc.scalar.activation(out=warm[:, 1:2], in_=warm[:, 0:1], func=SIGMOID)
        nc.vector.memset(x1_scales[:].bitcast(I32), 0)
        for h in range(HALVES):
            nc.vector.memset(ij_scales[h][:].bitcast(I32), 0)

        def transpose_two(rows_a, rows_b, grouped_words):
            bank = transpose_psum.tile([P, 2, 2, P], F32, name="bank", tag="bank")
            for block, rows in enumerate((rows_a, rows_b)):
                for u in range(2):
                    nc.tensor.transpose(bank[:, block, u, :], rows[:, u * P : (u + 1) * P], identity[:])
            nc.scalar.copy(out=grouped_words, in_=bank[:].rearrange("p j u r -> p j r u"))

        def regroup_weights(g, on_vector):
            dst = w_grouped[g][:].rearrange("p (c i) t -> p c t i", i=4)
            src = w_raw[g][:].rearrange("p t (c i) -> p c t i", i=4)
            if on_vector:
                nc.vector.tensor_copy(out=dst, in_=src)
            else:
                nc.scalar.copy(out=dst, in_=src)

        def quantise_weights(g):
            nc.vector.quantize_mx(
                out=w_codes[:, g, :].bitcast(FP8X4),
                scales=w_scales[:, g, :],
                in_=w_grouped[g][:].rearrange("p o t -> p (o t)"),
            )

        grouped_of = {}

        def transpose_slab(h, s):
            words = x2_sb[h][s][:].bitcast(F32)
            grouped_of[(h, s)] = grouped_pool.tile([P, SLAB, P, PACK], BF16, name="grouped", tag="grouped", align_bytes=64)
            grouped_words = grouped_of[(h, s)][:].bitcast(F32)
            for block in range(0, SLAB, 2):
                transpose_two(words[:, block, :], words[:, block + 1, :], grouped_words[:, block : block + 2, :, :])

        def quantise_slab(h, s):
            blocks = slice(s * SLAB, (s + 1) * SLAB)
            nc.vector.quantize_mx(
                out=ij_codes[h][:, blocks, :].rearrange("p j r -> p (j r)").bitcast(FP8X4),
                scales=ij_scales[h][:, blocks, :].rearrange("p j r -> p (j r)"),
                in_=grouped_of[(h, s)][:].rearrange("p j r t -> p (j r t)"),
            )

        def repeat_x1(h, lo, hi):
            for dst, src, run in ((xj_codes, x1_codes, HALF_SCENES), (xj_scales, x1_scales, SCALE_WORDS)):
                nc.vector.tensor_copy(
                    out=dst[h][:, lo:hi, :].bitcast(I32).rearrange("p j (i w) -> p j i w", w=run),
                    in_=src[:, h, lo * HALF_SCENES : hi * HALF_SCENES].bitcast(I32)
                    .rearrange("p (j w) -> p j w", w=run).unsqueeze(2).to_broadcast([P, hi - lo, OBJECTS, run]),
                )

        def swap_x2(h, lo, hi):
            for dst, src, run in ((ji_codes, ij_codes, HALF_SCENES), (ji_scales, ij_scales, SCALE_WORDS)):
                nc.vector.tensor_copy(
                    out=dst[h][:, lo:hi, :].bitcast(I32).rearrange("p j (i w) -> p j i w", w=run),
                    in_=src[h][:].bitcast(I32).rearrange("p i (j w) -> p j i w", w=run)[:, lo:hi, :, :],
                )

        def mx_pass(bank, codes, scales, g, start, stop):
            nc.tensor.matmul_mx(
                out=bank,
                lhsT=codes.bitcast(FP8X4),
                lhsT_scale=scales,
                rhs=w_codes[:, g, :].bitcast(FP8X4),
                rhs_scale=w_scales[:, g, :],
                start=start,
                stop=stop,
            )

        x1_banks = {}

        def x1_term_pass(h):
            x1_banks[h] = transpose_psum.tile([P, OUT], F32, name="x1_bank", tag="bank")
            mx_pass(x1_banks[h][:], x1_codes[:, h, :], x1_scales[:, h, :], W_X1_I, True, True)

        def x1_term_add(h):
            nc.vector.tensor_tensor(out=x1_term[h][:], in0=x1_banks[h][:], in1=bias_all[:], op=ADD)

        banks = {}

        def pass_ij(n):
            h, j = divmod(n, OBJECTS)
            banks[n] = tile_psum.tile([P, OUT], F32, name="tile_bank", tag="tile_bank")
            mx_pass(banks[n][:], ij_codes[h][:, j, :], ij_scales[h][:, j, :], W_X2_IJ, True, False)

        def pass_xj(n):
            h, j = divmod(n, OBJECTS)
            mx_pass(banks[n][:], xj_codes[h][:, j, :], xj_scales[h][:, j, :], W_X1_J, False, False)

        def pass_ji(n):
            h, j = divmod(n, OBJECTS)
            mx_pass(banks[n][:], ji_codes[h][:, j, :], ji_scales[h][:, j, :], W_X2_JI, False, True)

        store_of = {}
        first = 0
        for size in STORE_SIZES:
            for n in range(first, first + size):
                store_of[n] = (first, size)
            first += size
        results = {}

        def add_x1_term(n):
            first_n, size = store_of[n]
            if n == first_n:
                results[first_n] = result_pools[size].tile([P, size, OUT], F32, name="result", tag="result")
            nc.vector.tensor_tensor(
                out=results[first_n][:, n - first_n, :], in0=x1_term[n // OBJECTS][:], in1=banks[n][:], op=ADD
            )

        def sigmoid_and_store(n):
            first_n, size = store_of[n]
            part = results[first_n][:, n - first_n, :]
            nc.scalar.activation(out=part, in_=part, func=SIGMOID)
            if n == first_n + size - 1:
                h, j = divmod(n, OBJECTS)
                nc.sync.dma_start(
                    out=out_view[h][:, :, (j + 1 - size) * OUT : (j + 1) * OUT],
                    in_=results[first_n][:].rearrange("p j o -> p (j o)"),
                )

        x1_words = x1_sb[:].bitcast(F32)
        transpose_two(x1_words[:, 0, :], x1_words[:, 1, :], x1_grouped[:].bitcast(F32))
        regroup_weights(W_X2_IJ, True)
        nc.vector.quantize_mx(
            out=x1_codes[:].rearrange("p h r -> p (h r)").bitcast(FP8X4),
            scales=x1_scales[:].rearrange("p h r -> p (h r)"),
            in_=x1_grouped[:].rearrange("p h r t -> p (h r t)"),
        )
        quantise_weights(W_X2_IJ)
        regroup_weights(W_X1_J, False)
        for h in range(HALVES):
            repeat_x1(h, 0, OBJECTS)
        transpose_slab(0, 0)
        quantise_weights(W_X1_J)
        regroup_weights(W_X2_JI, True)
        quantise_slab(0, 0)
        transpose_slab(0, 1)
        quantise_weights(W_X2_JI)
        regroup_weights(W_X1_I, True)
        quantise_slab(0, 1)
        transpose_slab(0, 2)
        quantise_weights(W_X1_I)
        quantise_slab(0, 2)
        transpose_slab(0, 3)
        quantise_slab(0, 3)
        bias_bank = transpose_psum.tile([P, OUT], F32, name="bias_bank", tag="bank")
        nc.tensor.matmul(bias_bank[:], lhsT=ones[:], rhs=bias_row[:], start=True, stop=True)
        nc.scalar.copy(out=bias_all[:], in_=bias_bank[:])
        for n in range(TILE_BANKS):
            pass_ij(n)
        for n in range(TILE_BANKS):
            pass_xj(n)
        x1_term_pass(0)
        swap_x2(0, *SWAP_PIECES[0][0])
        x1_term_add(0)
        transpose_slab(1, 0)
        for n in range(TILE_BANKS):
            pass_ji(n)
        swap_x2(0, *SWAP_PIECES[0][1])

        for n in range(TILES):
            if n + 1 < SLABS:
                transpose_slab(1, n + 1)
            add_x1_term(n)
            if 1 <= n <= SLABS:
                quantise_slab(1, n - 1)
            if n == SECOND_X1_TERM_AFTER_TILE:
                x1_term_pass(1)
                x1_term_add(1)
            if n in SWAP_AFTER_TILE:
                swap_x2(1, *SWAP_PIECES[1][SWAP_AFTER_TILE.index(n)])
            sigmoid_and_store(n)
            ahead = n + TILE_BANKS
            if ahead < TILES:
                pass_ij(ahead)
                pass_xj(ahead)
                pass_ji(ahead)
